import numpy as np
import ml_dtypes


def mxq(x, axis, fmt="e4m3"):
    dtype, down = {"e4m3": (ml_dtypes.float8_e4m3fn, 7), "e5m2": (ml_dtypes.float8_e5m2, 14)}[fmt]
    v = np.moveaxis(np.asarray(x, np.float32).astype(ml_dtypes.bfloat16).astype(np.float64), axis, -1)
    blocks = v.reshape(v.shape[:-1] + (-1, 32))
    amax = np.abs(blocks).max(-1, keepdims=True)
    byte = np.maximum(np.where(amax > 0, np.frexp(amax)[1] - 1 + 127, 0) - down, 1)
    scale = np.exp2(byte - 127.0)
    codes = (blocks / scale).astype(np.float32).astype(dtype).astype(np.float64)
    return np.moveaxis((codes * scale).reshape(v.shape), -1, axis)


WIDE = False


def mx_kscale(k):
    if not WIDE:
        return np.ones(k)
    levels = np.array([10, -10, 5, -5, 0])
    a = np.random.permutation(np.resize(levels, k // 512 * 4)).reshape(k // 512, 4)
    idx = np.arange(k)
    return np.exp2(a[idx // 512, idx % 128 // 32])


BF16 = ml_dtypes.bfloat16


def bf(x):
    return np.asarray(x, np.float32).astype(BF16)


def f64(x):
    return np.asarray(x).astype(np.float64)


E2M1 = np.array([0.0, 0.5, 1.0, 1.5, 2.0, 3.0, 4.0, 6.0, -0.0, -0.5, -1.0, -1.5, -2.0, -3.0, -4.0, -6.0])


def pack_weight(w, fmt):
    k, n = w.shape
    w = f64(bf(w)).reshape(k // 32, 32, n)
    amax = np.abs(w).max(1)
    if fmt == "e4m3":
        byte = np.frexp(amax)[1] - 1 + 127 - 7
    else:
        mant, ex = np.frexp(amax / 6.0)
        byte = np.where(mant > 0.5, ex, ex - 1) + 127
    byte = np.clip(np.where(amax > 0, byte, 1), 1, 254)
    scaled = (w * np.exp2(127.0 - byte)[:, None, :]).reshape(k, n).astype(np.float32)
    by_word = np.ascontiguousarray(scaled.reshape(k // 512, 128, 4, n).transpose(0, 1, 3, 2))
    if fmt == "e4m3":
        words = by_word.astype(ml_dtypes.float8_e4m3fn).view(np.uint8)
    else:
        c = by_word.astype(ml_dtypes.float4_e2m1fn).view(np.uint8) & 0xF
        words = c[..., 0::2] | (c[..., 1::2] << 4)
    return np.ascontiguousarray(words), np.ascontiguousarray(byte.astype(np.uint8).reshape(k // 512, 16, n))


def unpack_weight(words, scales, fmt):
    g, p, n, _ = words.shape
    if fmt == "e4m3":
        vals = np.ascontiguousarray(words).view(ml_dtypes.float8_e4m3fn).astype(np.float64)
    else:
        nib = np.empty((g, p, n, 4), np.uint8)
        nib[..., 0::2] = words & 0xF
        nib[..., 1::2] = words >> 4
        vals = E2M1[nib]
    vals = vals * np.repeat(np.exp2(scales.astype(np.float64) - 127.0), 8, axis=1)[..., None]
    return vals.transpose(0, 1, 3, 2).reshape(g * 512, n)

def pack4(w):
    words, scales = pack_weight(w, "e2m1")
    return words.reshape(words.shape[0], 128, -1), scales


def unpack4(words, scales):
    return unpack_weight(words.reshape(words.shape[0], 128, -1, 2), scales, "e2m1")


B, S, HID, NH, HD, RD, RATIO = 1, 2048, 1024, 8, 128, 64, 4
THETA = 10000.0
HALF = RD // 2


def rope_tables(positions):
    inv_freq = 1.0 / THETA ** (np.arange(HALF) / HALF)
    ang = positions[:, None] * inv_freq[None, :]
    return np.cos(ang), np.sin(ang)


def rope_interleaved(x, cos, sin):
    nope, rope = x[..., :-RD], x[..., -RD:]
    pr = rope.reshape(rope.shape[:-1] + (HALF, 2))
    a, b = pr[..., 0], pr[..., 1]
    new = np.stack([a * cos - b * sin, a * sin + b * cos], axis=-1).reshape(rope.shape)
    return np.concatenate([nope, new], axis=-1)


def setup_inputs():
    s = mx_kscale(HID)
    hidden = bf(np.random.standard_normal((B, S, HID)) * s)
    wq_words, wq_scales = pack4(np.random.standard_normal((HID, NH * HD)) / np.sqrt(HID) / s[:, None])
    return {"hidden": hidden,
            "wq_words": wq_words,
            "wq_scales": wq_scales}


def reference(hidden, wq_words, wq_scales):
    q = mxq(f64(hidden), 2, "e4m3") @ unpack4(wq_words, wq_scales)
    q = q.reshape(B, S, NH, HD).transpose(0, 2, 1, 3)
    cq, sq = rope_tables(np.arange(S))
    return rope_interleaved(q, cq, sq)

@@ -1,0 +1,196 @@
+from contextlib import ExitStack
+
+import concourse.mybir as mybir
+from concourse.masks import make_identity
+
+F32 = mybir.dt.float32
+BF16 = mybir.dt.bfloat16
+I32 = mybir.dt.int32
+U32 = mybir.dt.uint32
+U8 = mybir.dt.uint8
+FP8X4 = mybir.dt.float8_e4m3fn_x4
+FP4X4 = mybir.dt.float4_e2m1fn_x4
+ALU = mybir.AluOpType
+ACT = mybir.ActivationFunctionType
+
+P = 128
+TOKENS = 2048
+HID = 1024
+HEADS = 8
+HEAD_DIM = 128
+ROT = 64
+PAIRS = ROT // 2
+THETA = 10000.0
+TWO_PI = 6.283185307179586
+
+TILES = TOKENS // P
+K_PASS = 4 * P
+PASSES = HID // K_PASS
+PASS_WORDS = K_PASS // 2
+HALF = HEADS * ROT
+PLAIN, ROTATED = 0, 1
+ROUND = 2
+ROUNDS = TILES // ROUND
+PSUM_BANKS = 8
+ROUND_MAGIC = 12582912.0
+
+FLOPS = 2 * TOKENS * HID * HEADS * HEAD_DIM
+
+
+def tile_deepseekv4attention_pb_kernel(tc, hidden, wq_words, wq_scales, out):
+    nc = tc.nc
+    x_rows = hidden.flatten_outer_dims().rearrange("(p j) k -> p j k", j=TILES)
+    out_rows = out.rearrange("b h t d -> (b h) t d").rearrange("h (p j) d -> p h j d", j=TILES)
+
+    with ExitStack() as stack:
+        keep = stack.enter_context(tc.tile_pool(name="keep", bufs=1))
+        stage = stack.enter_context(tc.tile_pool(name="stage", bufs=3))
+        xt_pool = stack.enter_context(tc.psum_pool(name="xt_pool", bufs=ROUND))
+        acc_pool = stack.enter_context(tc.psum_pool(name="acc_pool", bufs=PSUM_BANKS - ROUND))
+        stack.enter_context(tc.manual_schedule())
+
+        x_sb = [keep.tile([P, HID], BF16, name="x%d" % j) for j in range(TILES)]
+        w_raw = keep.tile([P, PASSES * 2 * HID], U8, name="w_raw")
+        s_raw = keep.tile([P, PASSES * HID], U8, name="s_raw")
+
+        nc.vector.memset(s_raw[:].bitcast(I32), 0)
+        for j in range(ROUND):
+            nc.sync.dma_start(out=x_sb[j][:], in_=x_rows[:, j, :])
+        scale_rows = wq_scales.bitcast(I32).rearrange("g q n -> q g n")
+        for quad in range(4):
+            nc.sync.dma_start(
+                out=s_raw[32 * quad : 32 * quad + 4, :].bitcast(I32).rearrange("q (g n) -> q g n", g=PASSES),
+                in_=scale_rows[4 * quad : 4 * quad + 4],
+            )
+        nc.sync.dma_start(
+            out=w_raw[:].bitcast(I32).rearrange("p (g n) -> p g n", g=PASSES),
+            in_=wq_words.bitcast(I32).rearrange("g p n -> p g n"),
+        )
+        for j in range(ROUND, TILES):
+            nc.sync.dma_start(out=x_sb[j][:], in_=x_rows[:, j, :])
+
+        token = keep.tile([P, TILES], I32, name="token")
+        nc.gpsimd.iota(token[:], pattern=[[1, TILES]], base=0, channel_multiplier=TILES)
+        ident = keep.tile([P, P], F32, name="ident")
+        make_identity(nc, ident[:])
+
+        turns = keep.tile([P, TILES, PAIRS], F32, name="turns")
+        for i in range(PAIRS):
+            nc.vector.tensor_scalar(
+                out=turns[:, :, i], in0=token[:], scalar1=THETA ** (-i / PAIRS) / TWO_PI, scalar2=None, op0=ALU.mult
+            )
+        whole = keep.tile([P, TILES, PAIRS], F32, name="whole")
+        nc.vector.tensor_scalar(
+            out=whole[:], in0=turns[:], scalar1=ROUND_MAGIC, scalar2=ROUND_MAGIC, op0=ALU.add, op1=ALU.subtract
+        )
+        sin_turn = keep.tile([P, TILES, PAIRS], F32, name="sin_turn")
+        nc.vector.tensor_tensor(out=sin_turn[:], in0=turns[:], in1=whole[:], op=ALU.subtract)
+        wraps = keep.tile([P, TILES, PAIRS], F32, name="wraps")
+        nc.vector.tensor_scalar(out=wraps[:], in0=sin_turn[:], scalar1=0.25, scalar2=None, op0=ALU.is_gt)
+        cos_turn = keep.tile([P, TILES, PAIRS], F32, name="cos_turn")
+        nc.vector.scalar_tensor_tensor(
+            out=cos_turn[:], in0=sin_turn[:], scalar=0.25, in1=wraps[:], op0=ALU.add, op1=ALU.subtract
+        )
+        table = keep.tile([P, TILES, 4, PAIRS], F32, name="table")
+        nc.scalar.activation(out=table[:, :, 1, :], in_=sin_turn[:], func=ACT.Sin, scale=-TWO_PI)
+        nc.scalar.activation(out=table[:, :, 2, :], in_=sin_turn[:], func=ACT.Sin, scale=TWO_PI)
+        nc.scalar.activation(
+            out=table[:, :, 0:4:3, :],
+            in_=cos_turn[:].unsqueeze(2).to_broadcast([P, TILES, 2, PAIRS]),
+            func=ACT.Sin,
+            scale=TWO_PI,
+        )
+
+        w_words = keep.tile([P, PASSES * 2 * HID], U8, name="w_words", align_bytes=64)
+        w_scales = keep.tile([P, PASSES * HID], U8, name="w_scales", align_bytes=64)
+        for g in range(PASSES):
+            for raw, ordered in ((w_raw, w_words), (s_raw, w_scales)):
+                width = raw.shape[1] // PASSES
+                nc.vector.tensor_copy(
+                    out=ordered[:, g * width : (g + 1) * width].bitcast(I32).rearrange("p (f h c) -> p f h c", f=2, h=HEADS),
+                    in_=raw[:, g * width : (g + 1) * width].bitcast(I32).rearrange("p (h f c) -> p f h c", f=2, h=HEADS),
+                )
+
+        xt_of, grouped_of, codes_of, planes_of, acc_of = {}, {}, {}, {}, {}
+
+        def transposes(r):
+            for a in range(ROUND):
+                words = x_sb[ROUND * r + a][:].bitcast(F32)
+                xt = xt_pool.tile([P, 2 * PASSES, P], F32, name="xt")
+                for g in range(PASSES):
+                    for u in range(2):
+                        nc.tensor.transpose(
+                            xt[:, 2 * g + u, :], words[:, PASS_WORDS * g + u : PASS_WORDS * (g + 1) : 2], ident[:]
+                        )
+                xt_of[r, a] = xt
+
+        def regroup(r):
+            grouped = stage.tile([P, ROUND * HID], BF16, name="grouped", align_bytes=64)
+            for a in range(ROUND):
+                nc.scalar.copy(
+                    out=grouped[:, a * HID : (a + 1) * HID].bitcast(F32).rearrange("p (g t u) -> p g t u", g=PASSES, u=2),
+                    in_=xt_of[r, a][:].rearrange("p (g u) t -> p g t u", u=2),
+                )
+            grouped_of[r] = grouped
+
+        def quantise(r):
+            codes = stage.tile([P, ROUND * PASSES * P], U32, name="codes", align_bytes=64)
+            planes = stage.tile([P, ROUND * PASSES * P], U8, name="planes", align_bytes=64)
+            nc.vector.quantize_mx(out=codes[:].bitcast(FP8X4), scales=planes[:], in_=grouped_of[r][:])
+            codes_of[r], planes_of[r] = codes, planes
+
+        def matmuls(r):
+            for a in range(ROUND):
+                for half in (ROTATED, PLAIN):
+                    acc = acc_pool.tile([P, HALF], F32, name="acc")
+                    for g in range(PASSES):
+                        tok = slice((a * PASSES + g) * P, (a * PASSES + g + 1) * P)
+                        col = g * 2 + half
+                        nc.tensor.matmul_mx(
+                            out=acc[:],
+                            lhsT=codes_of[r][:, tok].bitcast(FP8X4),
+                            lhsT_scale=planes_of[r][:, tok],
+                            rhs=w_words[:, col * 2 * HALF : (col + 1) * 2 * HALF].bitcast(FP4X4),
+                            rhs_scale=w_scales[:, col * HALF : (col + 1) * HALF],
+                            start=(g == 0),
+                            stop=(g == PASSES - 1),
+                        )
+                    acc_of[r, a, half] = acc
+
+        def finish(r):
+            res = stage.tile([P, HEADS, ROUND, HEAD_DIM], F32, name="res")
+            for a in range(ROUND):
+                products = stage.tile([P, 2, 2, HEADS, PAIRS], F32, name="products", bufs=4)
+                shape = [P, 2, 2, HEADS, PAIRS]
+                nc.vector.tensor_tensor(
+                    out=products[:],
+                    in0=acc_of[r, a, ROTATED][:].rearrange("p (h i e) -> p e h i", h=HEADS, e=2).unsqueeze(1).to_broadcast(shape),
+                    in1=table[:, ROUND * r + a, :, :].rearrange("p (o e) i -> p o e i", e=2).unsqueeze(3).to_broadcast(shape),
+                    op=ALU.mult,
+                )
+                nc.scalar.copy(
+                    out=res[:, :, a, 0 : HEAD_DIM - ROT],
+                    in_=acc_of[r, a, PLAIN][:].rearrange("p (h d) -> p h d", h=HEADS),
+                )
+                nc.gpsimd.tensor_tensor(
+                    out=res[:, :, a, HEAD_DIM - ROT : HEAD_DIM].rearrange("p h (i o) -> p h i o", o=2),
+                    in0=products[:, :, 0, :, :].rearrange("p o h i -> p h i o"),
+                    in1=products[:, :, 1, :, :].rearrange("p o h i -> p h i o"),
+                    op=ALU.add,
+                )
+            nc.sync.dma_start(out=out_rows[:, :, ROUND * r : ROUND * (r + 1), :], in_=res[:])
+
+        transposes(0)
+        regroup(0)
+        transposes(1)
+        regroup(1)
+        quantise(0)
+        for r in range(ROUNDS):
+            matmuls(r)
+            if r + 2 < ROUNDS:
+                transposes(r + 2)
+            if r + 1 < ROUNDS:
+                quantise(r + 1)
+            finish(r)
+            if r + 2 < ROUNDS:
+                regroup(r + 2)

@@ -32,6 +32,9 @@ PLAIN, ROTATED = 0, 1
 ROUND = 2
 ROUNDS = TILES // ROUND
 PSUM_BANKS = 8
+VECTOR_HEADS = 2
+LAST_VECTOR_HEADS = 4
+AHEAD = 2
 ROUND_MAGIC = 12582912.0
 
 FLOPS = 2 * TOKENS * HID * HEADS * HEAD_DIM
@@ -94,12 +97,6 @@ def tile_deepseekv4attention_pb_kernel(tc, hidden, wq_words, wq_scales, out):
         table = keep.tile([P, TILES, 4, PAIRS], F32, name="table")
         nc.scalar.activation(out=table[:, :, 1, :], in_=sin_turn[:], func=ACT.Sin, scale=-TWO_PI)
         nc.scalar.activation(out=table[:, :, 2, :], in_=sin_turn[:], func=ACT.Sin, scale=TWO_PI)
-        nc.scalar.activation(
-            out=table[:, :, 0:4:3, :],
-            in_=cos_turn[:].unsqueeze(2).to_broadcast([P, TILES, 2, PAIRS]),
-            func=ACT.Sin,
-            scale=TWO_PI,
-        )
 
         w_words = keep.tile([P, PASSES * 2 * HID], U8, name="w_words", align_bytes=64)
         w_scales = keep.tile([P, PASSES * HID], U8, name="w_scales", align_bytes=64)
@@ -125,7 +122,7 @@ def tile_deepseekv4attention_pb_kernel(tc, hidden, wq_words, wq_scales, out):
                 xt_of[r, a] = xt
 
         def regroup(r):
-            grouped = stage.tile([P, ROUND * HID], BF16, name="grouped", align_bytes=64)
+            grouped = stage.tile([P, ROUND * HID], BF16, name="grouped", align_bytes=64, bufs=AHEAD + 1)
             for a in range(ROUND):
                 nc.scalar.copy(
                     out=grouped[:, a * HID : (a + 1) * HID].bitcast(F32).rearrange("p (g t u) -> p g t u", g=PASSES, u=2),
@@ -159,38 +156,58 @@ def tile_deepseekv4attention_pb_kernel(tc, hidden, wq_words, wq_scales, out):
 
         def finish(r):
             res = stage.tile([P, HEADS, ROUND, HEAD_DIM], F32, name="res")
+            shape = [P, 2, 2, HEADS, PAIRS]
+            products_of = {}
             for a in range(ROUND):
-                products = stage.tile([P, 2, 2, HEADS, PAIRS], F32, name="products", bufs=4)
-                shape = [P, 2, 2, HEADS, PAIRS]
+                products = stage.tile(shape, F32, name="products", bufs=6)
                 nc.vector.tensor_tensor(
                     out=products[:],
                     in0=acc_of[r, a, ROTATED][:].rearrange("p (h i e) -> p e h i", h=HEADS, e=2).unsqueeze(1).to_broadcast(shape),
                     in1=table[:, ROUND * r + a, :, :].rearrange("p (o e) i -> p o e i", e=2).unsqueeze(3).to_broadcast(shape),
                     op=ALU.mult,
                 )
+                products_of[a] = products
+            for a in range(ROUND):
                 nc.scalar.copy(
                     out=res[:, :, a, 0 : HEAD_DIM - ROT],
                     in_=acc_of[r, a, PLAIN][:].rearrange("p (h d) -> p h d", h=HEADS),
                 )
-                nc.gpsimd.tensor_tensor(
-                    out=res[:, :, a, HEAD_DIM - ROT : HEAD_DIM].rearrange("p h (i o) -> p h i o", o=2),
-                    in0=products[:, :, 0, :, :].rearrange("p o h i -> p h i o"),
-                    in1=products[:, :, 1, :, :].rearrange("p o h i -> p h i o"),
+
+            def add_products(engine, a, heads):
+                engine.tensor_tensor(
+                    out=res[:, heads, a, HEAD_DIM - ROT : HEAD_DIM].rearrange("p h (i o) -> p h i o", o=2),
+                    in0=products_of[a][:, :, 0, heads, :].rearrange("p o h i -> p h i o"),
+                    in1=products_of[a][:, :, 1, heads, :].rearrange("p o h i -> p h i o"),
                     op=ALU.add,
                 )
-            nc.sync.dma_start(out=out_rows[:, :, ROUND * r : ROUND * (r + 1), :], in_=res[:])
+
+            vector_heads = LAST_VECTOR_HEADS if r == ROUNDS - 1 else VECTOR_HEADS
+            for a in range(ROUND):
+                add_products(nc.gpsimd, a, slice(0, HEADS - vector_heads))
+                add_products(nc.vector, a, slice(HEADS - vector_heads, HEADS))
+            step = ROUND if r < ROUNDS - 1 else 1
+            for a in range(0, ROUND, step):
+                j = ROUND * r + a
+                nc.sync.dma_start(out=out_rows[:, :, j : j + step, :], in_=res[:, :, a : a + step, :])
 
         transposes(0)
         regroup(0)
-        transposes(1)
-        regroup(1)
+        nc.scalar.activation(
+            out=table[:, :, 0:4:3, :],
+            in_=cos_turn[:].unsqueeze(2).to_broadcast([P, TILES, 2, PAIRS]),
+            func=ACT.Sin,
+            scale=TWO_PI,
+        )
+        for r in range(1, AHEAD):
+            transposes(r)
+            regroup(r)
         quantise(0)
         for r in range(ROUNDS):
             matmuls(r)
-            if r + 2 < ROUNDS:
-                transposes(r + 2)
+            if r + AHEAD < ROUNDS:
+                transposes(r + AHEAD)
             if r + 1 < ROUNDS:
                 quantise(r + 1)
             finish(r)
-            if r + 2 < ROUNDS:
-                regroup(r + 2)
+            if r + AHEAD < ROUNDS:
+                regroup(r + AHEAD)

@@ -32,7 +32,6 @@ PLAIN, ROTATED = 0, 1
 ROUND = 2
 ROUNDS = TILES // ROUND
 PSUM_BANKS = 8
-VECTOR_HEADS = 2
 LAST_VECTOR_HEADS = 4
 AHEAD = 2
 ROUND_MAGIC = 12582912.0
@@ -181,10 +180,11 @@ def tile_deepseekv4attention_pb_kernel(tc, hidden, wq_words, wq_scales, out):
                     op=ALU.add,
                 )
 
-            vector_heads = LAST_VECTOR_HEADS if r == ROUNDS - 1 else VECTOR_HEADS
+            vector_heads = LAST_VECTOR_HEADS if r == ROUNDS - 1 else 0
             for a in range(ROUND):
                 add_products(nc.gpsimd, a, slice(0, HEADS - vector_heads))
-                add_products(nc.vector, a, slice(HEADS - vector_heads, HEADS))
+                if vector_heads:
+                    add_products(nc.vector, a, slice(HEADS - vector_heads, HEADS))
             step = ROUND if r < ROUNDS - 1 else 1
             for a in range(0, ROUND, step):
                 j = ROUND * r + a

@@ -32,7 +32,8 @@ PLAIN, ROTATED = 0, 1
 ROUND = 2
 ROUNDS = TILES // ROUND
 PSUM_BANKS = 8
-LAST_VECTOR_HEADS = 4
+VECTOR_HEADS = 2
+PLAIN_LAG = 1
 AHEAD = 2
 ROUND_MAGIC = 12582912.0
 
@@ -107,7 +108,7 @@ def tile_deepseekv4attention_pb_kernel(tc, hidden, wq_words, wq_scales, out):
                     in_=raw[:, g * width : (g + 1) * width].bitcast(I32).rearrange("p (h f c) -> p f h c", f=2, h=HEADS),
                 )
 
-        xt_of, grouped_of, codes_of, planes_of, acc_of = {}, {}, {}, {}, {}
+        xt_of, grouped_of, codes_of, planes_of, acc_of, res_of = {}, {}, {}, {}, {}, {}
 
         def transposes(r):
             for a in range(ROUND):
@@ -130,61 +131,61 @@ def tile_deepseekv4attention_pb_kernel(tc, hidden, wq_words, wq_scales, out):
             grouped_of[r] = grouped
 
         def quantise(r):
-            codes = stage.tile([P, ROUND * PASSES * P], U32, name="codes", align_bytes=64)
-            planes = stage.tile([P, ROUND * PASSES * P], U8, name="planes", align_bytes=64)
+            codes = stage.tile([P, ROUND * PASSES * P], U32, name="codes", align_bytes=64, bufs=4)
+            planes = stage.tile([P, ROUND * PASSES * P], U8, name="planes", align_bytes=64, bufs=4)
             nc.vector.quantize_mx(out=codes[:].bitcast(FP8X4), scales=planes[:], in_=grouped_of[r][:])
             codes_of[r], planes_of[r] = codes, planes
 
-        def matmuls(r):
+        def matmuls(r, half):
             for a in range(ROUND):
-                for half in (ROTATED, PLAIN):
-                    acc = acc_pool.tile([P, HALF], F32, name="acc")
-                    for g in range(PASSES):
-                        tok = slice((a * PASSES + g) * P, (a * PASSES + g + 1) * P)
-                        col = g * 2 + half
-                        nc.tensor.matmul_mx(
-                            out=acc[:],
-                            lhsT=codes_of[r][:, tok].bitcast(FP8X4),
-                            lhsT_scale=planes_of[r][:, tok],
-                            rhs=w_words[:, col * 2 * HALF : (col + 1) * 2 * HALF].bitcast(FP4X4),
-                            rhs_scale=w_scales[:, col * HALF : (col + 1) * HALF],
-                            start=(g == 0),
-                            stop=(g == PASSES - 1),
-                        )
-                    acc_of[r, a, half] = acc
+                acc = acc_pool.tile([P, HALF], F32, name="acc")
+                for g in range(PASSES):
+                    tok = slice((a * PASSES + g) * P, (a * PASSES + g + 1) * P)
+                    col = g * 2 + half
+                    nc.tensor.matmul_mx(
+                        out=acc[:],
+                        lhsT=codes_of[r][:, tok].bitcast(FP8X4),
+                        lhsT_scale=planes_of[r][:, tok],
+                        rhs=w_words[:, col * 2 * HALF : (col + 1) * 2 * HALF].bitcast(FP4X4),
+                        rhs_scale=w_scales[:, col * HALF : (col + 1) * HALF],
+                        start=(g == 0),
+                        stop=(g == PASSES - 1),
+                    )
+                acc_of[r, a, half] = acc
 
-        def finish(r):
-            res = stage.tile([P, HEADS, ROUND, HEAD_DIM], F32, name="res")
-            shape = [P, 2, 2, HEADS, PAIRS]
+        def rotate(r):
+            res = stage.tile([P, HEADS, ROUND, HEAD_DIM], F32, name="res", bufs=4)
+            res_of[r] = res
+            shape = [P, HEADS, PAIRS, 2]
             products_of = {}
             for a in range(ROUND):
-                products = stage.tile(shape, F32, name="products", bufs=6)
-                nc.vector.tensor_tensor(
-                    out=products[:],
-                    in0=acc_of[r, a, ROTATED][:].rearrange("p (h i e) -> p e h i", h=HEADS, e=2).unsqueeze(1).to_broadcast(shape),
-                    in1=table[:, ROUND * r + a, :, :].rearrange("p (o e) i -> p o e i", e=2).unsqueeze(3).to_broadcast(shape),
-                    op=ALU.mult,
-                )
+                products = stage.tile([P, 2] + shape[1:], F32, name="products", bufs=6)
+                inputs = acc_of[r, a, ROTATED][:].rearrange("p (h i e) -> p e h i", h=HEADS, e=2)
+                factors = table[:, ROUND * r + a, :, :].rearrange("p (o e) i -> p e i o", e=2)
+                for e in range(2):
+                    nc.vector.tensor_tensor(
+                        out=products[:, e],
+                        in0=inputs[:, e].unsqueeze(3).to_broadcast(shape),
+                        in1=factors[:, e].unsqueeze(1).to_broadcast(shape),
+                        op=ALU.mult,
+                    )
                 products_of[a] = products
+            for a in range(ROUND):
+                for engine, heads in ((nc.gpsimd, slice(0, HEADS - VECTOR_HEADS)), (nc.vector, slice(HEADS - VECTOR_HEADS, HEADS))):
+                    engine.tensor_tensor(
+                        out=res[:, heads, a, HEAD_DIM - ROT : HEAD_DIM],
+                        in0=products_of[a][:, 0, heads].rearrange("p h i o -> p h (i o)"),
+                        in1=products_of[a][:, 1, heads].rearrange("p h i o -> p h (i o)"),
+                        op=ALU.add,
+                    )
+
+        def copy_and_store(r):
+            res = res_of[r]
             for a in range(ROUND):
                 nc.scalar.copy(
                     out=res[:, :, a, 0 : HEAD_DIM - ROT],
                     in_=acc_of[r, a, PLAIN][:].rearrange("p (h d) -> p h d", h=HEADS),
                 )
-
-            def add_products(engine, a, heads):
-                engine.tensor_tensor(
-                    out=res[:, heads, a, HEAD_DIM - ROT : HEAD_DIM].rearrange("p h (i o) -> p h i o", o=2),
-                    in0=products_of[a][:, :, 0, heads, :].rearrange("p o h i -> p h i o"),
-                    in1=products_of[a][:, :, 1, heads, :].rearrange("p o h i -> p h i o"),
-                    op=ALU.add,
-                )
-
-            vector_heads = LAST_VECTOR_HEADS if r == ROUNDS - 1 else 0
-            for a in range(ROUND):
-                add_products(nc.gpsimd, a, slice(0, HEADS - vector_heads))
-                if vector_heads:
-                    add_products(nc.vector, a, slice(HEADS - vector_heads, HEADS))
             step = ROUND if r < ROUNDS - 1 else 1
             for a in range(0, ROUND, step):
                 j = ROUND * r + a
@@ -202,12 +203,18 @@ def tile_deepseekv4attention_pb_kernel(tc, hidden, wq_words, wq_scales, out):
             transposes(r)
             regroup(r)
         quantise(0)
-        for r in range(ROUNDS):
-            matmuls(r)
+        for r in range(ROUNDS + PLAIN_LAG):
+            if r < ROUNDS:
+                matmuls(r, ROTATED)
+            if r >= PLAIN_LAG:
+                matmuls(r - PLAIN_LAG, PLAIN)
             if r + AHEAD < ROUNDS:
                 transposes(r + AHEAD)
             if r + 1 < ROUNDS:
                 quantise(r + 1)
-            finish(r)
+            if r < ROUNDS:
+                rotate(r)
+            if r >= PLAIN_LAG:
+                copy_and_store(r - PLAIN_LAG)
             if r + AHEAD < ROUNDS:
                 regroup(r + AHEAD)

@@ -32,8 +32,7 @@ PLAIN, ROTATED = 0, 1
 ROUND = 2
 ROUNDS = TILES // ROUND
 PSUM_BANKS = 8
-VECTOR_HEADS = 2
-PLAIN_LAG = 1
+LAST_VECTOR_HEADS = 4
 AHEAD = 2
 ROUND_MAGIC = 12582912.0
 
@@ -95,18 +94,35 @@ def tile_deepseekv4attention_pb_kernel(tc, hidden, wq_words, wq_scales, out):
             out=cos_turn[:], in0=sin_turn[:], scalar=0.25, in1=wraps[:], op0=ALU.add, op1=ALU.subtract
         )
         table = keep.tile([P, TILES, 4, PAIRS], F32, name="table")
-        nc.scalar.activation(out=table[:, :, 1, :], in_=sin_turn[:], func=ACT.Sin, scale=-TWO_PI)
-        nc.scalar.activation(out=table[:, :, 2, :], in_=sin_turn[:], func=ACT.Sin, scale=TWO_PI)
+
+        def sin_planes(tiles):
+            nc.scalar.activation(out=table[:, tiles, 1, :], in_=sin_turn[:, tiles, :], func=ACT.Sin, scale=-TWO_PI)
+            nc.scalar.activation(out=table[:, tiles, 2, :], in_=sin_turn[:, tiles, :], func=ACT.Sin, scale=TWO_PI)
+
+        def cos_planes(tiles):
+            nc.scalar.activation(
+                out=table[:, tiles, 0:4:3, :],
+                in_=cos_turn[:, tiles, :].unsqueeze(2).to_broadcast([P, TILES // 2, 2, PAIRS]),
+                func=ACT.Sin,
+                scale=TWO_PI,
+            )
+
+        early, late = slice(0, TILES // 2), slice(TILES // 2, TILES)
 
         w_words = keep.tile([P, PASSES * 2 * HID], U8, name="w_words", align_bytes=64)
         w_scales = keep.tile([P, PASSES * HID], U8, name="w_scales", align_bytes=64)
-        for g in range(PASSES):
-            for raw, ordered in ((w_raw, w_words), (s_raw, w_scales)):
-                width = raw.shape[1] // PASSES
-                nc.vector.tensor_copy(
-                    out=ordered[:, g * width : (g + 1) * width].bitcast(I32).rearrange("p (f h c) -> p f h c", f=2, h=HEADS),
-                    in_=raw[:, g * width : (g + 1) * width].bitcast(I32).rearrange("p (h f c) -> p f h c", f=2, h=HEADS),
-                )
+
+        def order_columns(half):
+            for g in range(PASSES):
+                for raw, ordered in ((w_raw, w_words), (s_raw, w_scales)):
+                    width = raw.shape[1] // (2 * PASSES)
+                    col = g * 2 + half
+                    nc.vector.tensor_copy(
+                        out=ordered[:, col * width : (col + 1) * width].bitcast(I32).rearrange("p (h c) -> p h c", h=HEADS),
+                        in_=raw[:, g * 2 * width : (g + 1) * 2 * width]
+                        .bitcast(I32)
+                        .rearrange("p (h f c) -> p f h c", f=2, h=HEADS)[:, half],
+                    )
 
         xt_of, grouped_of, codes_of, planes_of, acc_of, res_of = {}, {}, {}, {}, {}, {}
 
@@ -170,14 +186,20 @@ def tile_deepseekv4attention_pb_kernel(tc, hidden, wq_words, wq_scales, out):
                         op=ALU.mult,
                     )
                 products_of[a] = products
+
+            def add_products(engine, a, heads):
+                engine.tensor_tensor(
+                    out=res[:, heads, a, HEAD_DIM - ROT : HEAD_DIM],
+                    in0=products_of[a][:, 0, heads].rearrange("p h i o -> p h (i o)"),
+                    in1=products_of[a][:, 1, heads].rearrange("p h i o -> p h (i o)"),
+                    op=ALU.add,
+                )
+
+            vector_heads = LAST_VECTOR_HEADS if r == ROUNDS - 1 else 0
             for a in range(ROUND):
-                for engine, heads in ((nc.gpsimd, slice(0, HEADS - VECTOR_HEADS)), (nc.vector, slice(HEADS - VECTOR_HEADS, HEADS))):
-                    engine.tensor_tensor(
-                        out=res[:, heads, a, HEAD_DIM - ROT : HEAD_DIM],
-                        in0=products_of[a][:, 0, heads].rearrange("p h i o -> p h (i o)"),
-                        in1=products_of[a][:, 1, heads].rearrange("p h i o -> p h (i o)"),
-                        op=ALU.add,
-                    )
+                add_products(nc.gpsimd, a, slice(0, HEADS - vector_heads))
+                if vector_heads:
+                    add_products(nc.vector, a, slice(HEADS - vector_heads, HEADS))
 
         def copy_and_store(r):
             res = res_of[r]
@@ -186,35 +208,27 @@ def tile_deepseekv4attention_pb_kernel(tc, hidden, wq_words, wq_scales, out):
                     out=res[:, :, a, 0 : HEAD_DIM - ROT],
                     in_=acc_of[r, a, PLAIN][:].rearrange("p (h d) -> p h d", h=HEADS),
                 )
-            step = ROUND if r < ROUNDS - 1 else 1
-            for a in range(0, ROUND, step):
-                j = ROUND * r + a
-                nc.sync.dma_start(out=out_rows[:, :, j : j + step, :], in_=res[:, :, a : a + step, :])
+            nc.sync.dma_start(out=out_rows[:, :, ROUND * r : ROUND * (r + 1), :], in_=res[:])
 
+        sin_planes(early)
+        order_columns(ROTATED)
         transposes(0)
         regroup(0)
-        nc.scalar.activation(
-            out=table[:, :, 0:4:3, :],
-            in_=cos_turn[:].unsqueeze(2).to_broadcast([P, TILES, 2, PAIRS]),
-            func=ACT.Sin,
-            scale=TWO_PI,
-        )
+        cos_planes(early)
+        quantise(0)
+        order_columns(PLAIN)
         for r in range(1, AHEAD):
             transposes(r)
             regroup(r)
-        quantise(0)
-        for r in range(ROUNDS + PLAIN_LAG):
-            if r < ROUNDS:
-                matmuls(r, ROTATED)
-            if r >= PLAIN_LAG:
-                matmuls(r - PLAIN_LAG, PLAIN)
+        sin_planes(late)
+        cos_planes(late)
+        for r in range(ROUNDS):
+            matmuls(r, ROTATED)
             if r + AHEAD < ROUNDS:
                 transposes(r + AHEAD)
+                regroup(r + AHEAD)
+            matmuls(r, PLAIN)
             if r + 1 < ROUNDS:
                 quantise(r + 1)
-            if r < ROUNDS:
-                rotate(r)
-            if r >= PLAIN_LAG:
-                copy_and_store(r - PLAIN_LAG)
-            if r + AHEAD < ROUNDS:
-                regroup(r + AHEAD)
+            rotate(r)
+            copy_and_store(r)

@@ -169,37 +169,41 @@ def tile_deepseekv4attention_pb_kernel(tc, hidden, wq_words, wq_scales, out):
                     )
                 acc_of[r, a, half] = acc
 
-        def rotate(r):
-            res = stage.tile([P, HEADS, ROUND, HEAD_DIM], F32, name="res", bufs=4)
-            res_of[r] = res
+        products_of = {}
+
+        def multiply(r, a):
             shape = [P, HEADS, PAIRS, 2]
-            products_of = {}
-            for a in range(ROUND):
-                products = stage.tile([P, 2] + shape[1:], F32, name="products", bufs=6)
-                inputs = acc_of[r, a, ROTATED][:].rearrange("p (h i e) -> p e h i", h=HEADS, e=2)
-                factors = table[:, ROUND * r + a, :, :].rearrange("p (o e) i -> p e i o", e=2)
-                for e in range(2):
-                    nc.vector.tensor_tensor(
-                        out=products[:, e],
-                        in0=inputs[:, e].unsqueeze(3).to_broadcast(shape),
-                        in1=factors[:, e].unsqueeze(1).to_broadcast(shape),
-                        op=ALU.mult,
-                    )
-                products_of[a] = products
-
-            def add_products(engine, a, heads):
-                engine.tensor_tensor(
-                    out=res[:, heads, a, HEAD_DIM - ROT : HEAD_DIM],
-                    in0=products_of[a][:, 0, heads].rearrange("p h i o -> p h (i o)"),
-                    in1=products_of[a][:, 1, heads].rearrange("p h i o -> p h (i o)"),
-                    op=ALU.add,
+            products = stage.tile([P, 2] + shape[1:], F32, name="products", bufs=6)
+            inputs = acc_of[r, a, ROTATED][:].rearrange("p (h i e) -> p e h i", h=HEADS, e=2)
+            factors = table[:, ROUND * r + a, :, :].rearrange("p (o e) i -> p e i o", e=2)
+            for e in range(2):
+                nc.vector.tensor_tensor(
+                    out=products[:, e],
+                    in0=inputs[:, e].unsqueeze(3).to_broadcast(shape),
+                    in1=factors[:, e].unsqueeze(1).to_broadcast(shape),
+                    op=ALU.mult,
                 )
+            products_of[r, a] = products
 
+        def add_products(engine, r, a, heads):
+            engine.tensor_tensor(
+                out=res_of[r][:, heads, a, HEAD_DIM - ROT : HEAD_DIM],
+                in0=products_of[r, a][:, 0, heads].rearrange("p h i o -> p h (i o)"),
+                in1=products_of[r, a][:, 1, heads].rearrange("p h i o -> p h (i o)"),
+                op=ALU.add,
+            )
+
+        def rotate(r):
+            res_of[r] = stage.tile([P, HEADS, ROUND, HEAD_DIM], F32, name="res", bufs=4)
             vector_heads = LAST_VECTOR_HEADS if r == ROUNDS - 1 else 0
             for a in range(ROUND):
-                add_products(nc.gpsimd, a, slice(0, HEADS - vector_heads))
-                if vector_heads:
-                    add_products(nc.vector, a, slice(HEADS - vector_heads, HEADS))
+                multiply(r, a)
+                if a == 0 and r + 1 < ROUNDS:
+                    quantise(r + 1)
+                add_products(nc.gpsimd, r, a, slice(0, HEADS - vector_heads))
+            if vector_heads:
+                for a in range(ROUND):
+                    add_products(nc.vector, r, a, slice(HEADS - vector_heads, HEADS))
 
         def copy_and_store(r):
             res = res_of[r]
@@ -228,7 +232,5 @@ def tile_deepseekv4attention_pb_kernel(tc, hidden, wq_words, wq_scales, out):
                 transposes(r + AHEAD)
                 regroup(r + AHEAD)
             matmuls(r, PLAIN)
-            if r + 1 < ROUNDS:
-                quantise(r + 1)
             rotate(r)
             copy_and_store(r)

@@ -51,13 +51,13 @@ def tile_deepseekv4attention_pb_kernel(tc, hidden, wq_words, wq_scales, out):
         acc_pool = stack.enter_context(tc.psum_pool(name="acc_pool", bufs=PSUM_BANKS - ROUND))
         stack.enter_context(tc.manual_schedule())
 
-        x_sb = [keep.tile([P, HID], BF16, name="x%d" % j) for j in range(TILES)]
+        x_sb = [keep.tile([P, ROUND, HID], BF16, name="x%d" % r) for r in range(ROUNDS)]
         w_raw = keep.tile([P, PASSES * 2 * HID], U8, name="w_raw")
         s_raw = keep.tile([P, PASSES * HID], U8, name="s_raw")
 
         nc.vector.memset(s_raw[:].bitcast(I32), 0)
         for j in range(ROUND):
-            nc.sync.dma_start(out=x_sb[j][:], in_=x_rows[:, j, :])
+            nc.sync.dma_start(out=x_sb[0][:, j, :], in_=x_rows[:, j, :])
         scale_rows = wq_scales.bitcast(I32).rearrange("g q n -> q g n")
         for quad in range(4):
             nc.sync.dma_start(
@@ -68,8 +68,8 @@ def tile_deepseekv4attention_pb_kernel(tc, hidden, wq_words, wq_scales, out):
             out=w_raw[:].bitcast(I32).rearrange("p (g n) -> p g n", g=PASSES),
             in_=wq_words.bitcast(I32).rearrange("g p n -> p g n"),
         )
-        for j in range(ROUND, TILES):
-            nc.sync.dma_start(out=x_sb[j][:], in_=x_rows[:, j, :])
+        for r in range(1, ROUNDS):
+            nc.sync.dma_start(out=x_sb[r][:], in_=x_rows[:, ROUND * r : ROUND * (r + 1), :])
 
         token = keep.tile([P, TILES], I32, name="token")
         nc.gpsimd.iota(token[:], pattern=[[1, TILES]], base=0, channel_multiplier=TILES)
@@ -128,7 +128,7 @@ def tile_deepseekv4attention_pb_kernel(tc, hidden, wq_words, wq_scales, out):
 
         def transposes(r):
             for a in range(ROUND):
-                words = x_sb[ROUND * r + a][:].bitcast(F32)
+                words = x_sb[r][:, a, :].bitcast(F32)
                 xt = xt_pool.tile([P, 2 * PASSES, P], F32, name="xt")
                 for g in range(PASSES):
                     for u in range(2):

@@ -32,8 +32,9 @@ PLAIN, ROTATED = 0, 1
 ROUND = 2
 ROUNDS = TILES // ROUND
 PSUM_BANKS = 8
-LAST_VECTOR_HEADS = 4
+STORE_HALVES = [slice(0, HEADS // 2), slice(HEADS // 2, HEADS)]
 AHEAD = 2
+BASE_PAIRS = 8
 ROUND_MAGIC = 12582912.0
 
 FLOPS = 2 * TOKENS * HID * HEADS * HEAD_DIM
@@ -58,6 +59,7 @@ def tile_deepseekv4attention_pb_kernel(tc, hidden, wq_words, wq_scales, out):
         nc.vector.memset(s_raw[:].bitcast(I32), 0)
         for j in range(ROUND):
             nc.sync.dma_start(out=x_sb[0][:, j, :], in_=x_rows[:, j, :])
+        nc.sync.dma_start(out=x_sb[1][:], in_=x_rows[:, ROUND : 2 * ROUND, :])
         scale_rows = wq_scales.bitcast(I32).rearrange("g q n -> q g n")
         for quad in range(4):
             nc.sync.dma_start(
@@ -68,7 +70,7 @@ def tile_deepseekv4attention_pb_kernel(tc, hidden, wq_words, wq_scales, out):
             out=w_raw[:].bitcast(I32).rearrange("p (g n) -> p g n", g=PASSES),
             in_=wq_words.bitcast(I32).rearrange("g p n -> p g n"),
         )
-        for r in range(1, ROUNDS):
+        for r in range(2, ROUNDS):
             nc.sync.dma_start(out=x_sb[r][:], in_=x_rows[:, ROUND * r : ROUND * (r + 1), :])
 
         token = keep.tile([P, TILES], I32, name="token")
@@ -77,10 +79,20 @@ def tile_deepseekv4attention_pb_kernel(tc, hidden, wq_words, wq_scales, out):
         make_identity(nc, ident[:])
 
         turns = keep.tile([P, TILES, PAIRS], F32, name="turns")
-        for i in range(PAIRS):
+        for i in range(BASE_PAIRS):
             nc.vector.tensor_scalar(
                 out=turns[:, :, i], in0=token[:], scalar1=THETA ** (-i / PAIRS) / TWO_PI, scalar2=None, op0=ALU.mult
             )
+        done = BASE_PAIRS
+        while done < PAIRS:
+            nc.vector.tensor_scalar(
+                out=turns[:, :, done : 2 * done],
+                in0=turns[:, :, 0:done],
+                scalar1=THETA ** (-done / PAIRS),
+                scalar2=None,
+                op0=ALU.mult,
+            )
+            done *= 2
         whole = keep.tile([P, TILES, PAIRS], F32, name="whole")
         nc.vector.tensor_scalar(
             out=whole[:], in0=turns[:], scalar1=ROUND_MAGIC, scalar2=ROUND_MAGIC, op0=ALU.add, op1=ALU.subtract
@@ -170,20 +182,21 @@ def tile_deepseekv4attention_pb_kernel(tc, hidden, wq_words, wq_scales, out):
                 acc_of[r, a, half] = acc
 
         products_of = {}
+        all_heads = slice(0, HEADS)
 
-        def multiply(r, a):
-            shape = [P, HEADS, PAIRS, 2]
-            products = stage.tile([P, 2] + shape[1:], F32, name="products", bufs=6)
+        def multiply(r, a, heads):
+            if (r, a) not in products_of:
+                products_of[r, a] = stage.tile([P, 2, HEADS, PAIRS, 2], F32, name="products", bufs=6)
+            shape = [P, heads.stop - heads.start, PAIRS, 2]
             inputs = acc_of[r, a, ROTATED][:].rearrange("p (h i e) -> p e h i", h=HEADS, e=2)
             factors = table[:, ROUND * r + a, :, :].rearrange("p (o e) i -> p e i o", e=2)
             for e in range(2):
                 nc.vector.tensor_tensor(
-                    out=products[:, e],
-                    in0=inputs[:, e].unsqueeze(3).to_broadcast(shape),
+                    out=products_of[r, a][:, e, heads],
+                    in0=inputs[:, e, heads].unsqueeze(3).to_broadcast(shape),
                     in1=factors[:, e].unsqueeze(1).to_broadcast(shape),
                     op=ALU.mult,
                 )
-            products_of[r, a] = products
 
         def add_products(engine, r, a, heads):
             engine.tensor_tensor(
@@ -194,32 +207,37 @@ def tile_deepseekv4attention_pb_kernel(tc, hidden, wq_words, wq_scales, out):
             )
 
         def rotate(r):
-            res_of[r] = stage.tile([P, HEADS, ROUND, HEAD_DIM], F32, name="res", bufs=4)
-            vector_heads = LAST_VECTOR_HEADS if r == ROUNDS - 1 else 0
             for a in range(ROUND):
-                multiply(r, a)
-                if a == 0 and r + 1 < ROUNDS:
+                multiply(r, a, all_heads)
+                if a == 0 and r + 1 < ROUNDS - 1:
                     quantise(r + 1)
-                add_products(nc.gpsimd, r, a, slice(0, HEADS - vector_heads))
-            if vector_heads:
-                for a in range(ROUND):
-                    add_products(nc.vector, r, a, slice(HEADS - vector_heads, HEADS))
+                add_products(nc.gpsimd, r, a, all_heads)
+            if r == ROUNDS - 3:
+                quantise(ROUNDS - 1)
 
-        def copy_and_store(r):
-            res = res_of[r]
+        def rotate_last(r):
+            for half in STORE_HALVES:
+                for a in range(ROUND):
+                    multiply(r, a, half)
+                    last = half == STORE_HALVES[-1] and a == ROUND - 1
+                    add_products(nc.vector if last else nc.gpsimd, r, a, half)
+
+        def copy_plain(r):
             for a in range(ROUND):
                 nc.scalar.copy(
-                    out=res[:, :, a, 0 : HEAD_DIM - ROT],
+                    out=res_of[r][:, :, a, 0 : HEAD_DIM - ROT],
                     in_=acc_of[r, a, PLAIN][:].rearrange("p (h d) -> p h d", h=HEADS),
                 )
-            nc.sync.dma_start(out=out_rows[:, :, ROUND * r : ROUND * (r + 1), :], in_=res[:])
+
+        def store(r, heads):
+            nc.sync.dma_start(out=out_rows[:, heads, ROUND * r : ROUND * (r + 1), :], in_=res_of[r][:, heads])
 
         sin_planes(early)
-        order_columns(ROTATED)
+        cos_planes(early)
         transposes(0)
         regroup(0)
-        cos_planes(early)
         quantise(0)
+        order_columns(ROTATED)
         order_columns(PLAIN)
         for r in range(1, AHEAD):
             transposes(r)
@@ -227,10 +245,20 @@ def tile_deepseekv4attention_pb_kernel(tc, hidden, wq_words, wq_scales, out):
         sin_planes(late)
         cos_planes(late)
         for r in range(ROUNDS):
-            matmuls(r, ROTATED)
+            last = r == ROUNDS - 1
+            res_of[r] = stage.tile([P, HEADS, ROUND, HEAD_DIM], F32, name="res", bufs=4)
+            if not last:
+                matmuls(r, ROTATED)
+            if r == ROUNDS - 2:
+                matmuls(r + 1, ROTATED)
             if r + AHEAD < ROUNDS:
                 transposes(r + AHEAD)
                 regroup(r + AHEAD)
             matmuls(r, PLAIN)
-            rotate(r)
-            copy_and_store(r)
+            if last:
+                rotate_last(r)
+            else:
+                rotate(r)
+            copy_plain(r)
+            for heads in STORE_HALVES if last else [all_heads]:
+                store(r, heads)

@@ -33,6 +33,7 @@ ROUND = 2
 ROUNDS = TILES // ROUND
 PSUM_BANKS = 8
 STORE_HALVES = [slice(0, HEADS // 2), slice(HEADS // 2, HEADS)]
+EARLY_TILES = 4
 AHEAD = 2
 BASE_PAIRS = 8
 ROUND_MAGIC = 12582912.0
@@ -78,6 +79,10 @@ def tile_deepseekv4attention_pb_kernel(tc, hidden, wq_words, wq_scales, out):
         ident = keep.tile([P, P], F32, name="ident")
         make_identity(nc, ident[:])
 
+        first_sin = keep.tile([P, 1], F32, name="first_sin")
+        nc.gpsimd.memset(first_sin[:], 0.0)
+        nc.scalar.activation(out=first_sin[:], in_=first_sin[:], func=ACT.Sin)
+
         turns = keep.tile([P, TILES, PAIRS], F32, name="turns")
         for i in range(BASE_PAIRS):
             nc.vector.tensor_scalar(
@@ -114,12 +119,12 @@ def tile_deepseekv4attention_pb_kernel(tc, hidden, wq_words, wq_scales, out):
         def cos_planes(tiles):
             nc.scalar.activation(
                 out=table[:, tiles, 0:4:3, :],
-                in_=cos_turn[:, tiles, :].unsqueeze(2).to_broadcast([P, TILES // 2, 2, PAIRS]),
+                in_=cos_turn[:, tiles, :].unsqueeze(2).to_broadcast([P, tiles.stop - tiles.start, 2, PAIRS]),
                 func=ACT.Sin,
                 scale=TWO_PI,
             )
 
-        early, late = slice(0, TILES // 2), slice(TILES // 2, TILES)
+        early, late = slice(0, EARLY_TILES), slice(EARLY_TILES, TILES)
 
         w_words = keep.tile([P, PASSES * 2 * HID], U8, name="w_words", align_bytes=64)
         w_scales = keep.tile([P, PASSES * HID], U8, name="w_scales", align_bytes=64)
@@ -219,8 +224,7 @@ def tile_deepseekv4attention_pb_kernel(tc, hidden, wq_words, wq_scales, out):
             for half in STORE_HALVES:
                 for a in range(ROUND):
                     multiply(r, a, half)
-                    last = half == STORE_HALVES[-1] and a == ROUND - 1
-                    add_products(nc.vector if last else nc.gpsimd, r, a, half)
+                    add_products(nc.gpsimd if half == STORE_HALVES[0] else nc.vector, r, a, half)
 
         def copy_plain(r):
             for a in range(ROUND):
@@ -232,20 +236,21 @@ def tile_deepseekv4attention_pb_kernel(tc, hidden, wq_words, wq_scales, out):
         def store(r, heads):
             nc.sync.dma_start(out=out_rows[:, heads, ROUND * r : ROUND * (r + 1), :], in_=res_of[r][:, heads])
 
-        sin_planes(early)
-        cos_planes(early)
         transposes(0)
         regroup(0)
+        sin_planes(early)
+        cos_planes(early)
         quantise(0)
         order_columns(ROTATED)
         order_columns(PLAIN)
         for r in range(1, AHEAD):
             transposes(r)
             regroup(r)
-        sin_planes(late)
-        cos_planes(late)
         for r in range(ROUNDS):
             last = r == ROUNDS - 1
+            if r == 1:
+                sin_planes(late)
+                cos_planes(late)
             res_of[r] = stage.tile([P, HEADS, ROUND, HEAD_DIM], F32, name="res", bufs=4)
             if not last:
                 matmuls(r, ROTATED)

@@ -34,6 +34,7 @@ ROUNDS = TILES // ROUND
 PSUM_BANKS = 8
 STORE_HALVES = [slice(0, HEADS // 2), slice(HEADS // 2, HEADS)]
 EARLY_TILES = 4
+WARM_FIRST, WARM_BETWEEN = 4, 1
 AHEAD = 2
 BASE_PAIRS = 8
 ROUND_MAGIC = 12582912.0
@@ -82,6 +83,9 @@ def tile_deepseekv4attention_pb_kernel(tc, hidden, wq_words, wq_scales, out):
         first_sin = keep.tile([P, 1], F32, name="first_sin")
         nc.gpsimd.memset(first_sin[:], 0.0)
         nc.scalar.activation(out=first_sin[:], in_=first_sin[:], func=ACT.Sin)
+
+        zeros = keep.tile([P, HALF], BF16, name="zeros")
+        nc.gpsimd.memset(zeros[:].bitcast(I32), 0)
 
         turns = keep.tile([P, TILES, PAIRS], F32, name="turns")
         for i in range(BASE_PAIRS):
@@ -142,6 +146,12 @@ def tile_deepseekv4attention_pb_kernel(tc, hidden, wq_words, wq_scales, out):
                     )
 
         xt_of, grouped_of, codes_of, planes_of, acc_of, res_of = {}, {}, {}, {}, {}, {}
+
+        warm = acc_pool.tile([P, HALF], F32, name="acc")
+
+        def warm_up(count):
+            for turn in range(count):
+                nc.tensor.matmul(warm[:], lhsT=zeros[:, 0:P], rhs=zeros[:], start=True, stop=True)
 
         def transposes(r):
             for a in range(ROUND):
@@ -236,7 +246,9 @@ def tile_deepseekv4attention_pb_kernel(tc, hidden, wq_words, wq_scales, out):
         def store(r, heads):
             nc.sync.dma_start(out=out_rows[:, heads, ROUND * r : ROUND * (r + 1), :], in_=res_of[r][:, heads])
 
+        warm_up(WARM_FIRST)
         transposes(0)
+        warm_up(WARM_BETWEEN)
         regroup(0)
         sin_planes(early)
         cos_planes(early)
@@ -245,6 +257,7 @@ def tile_deepseekv4attention_pb_kernel(tc, hidden, wq_words, wq_scales, out):
         order_columns(PLAIN)
         for r in range(1, AHEAD):
             transposes(r)
+            warm_up(WARM_BETWEEN)
             regroup(r)
         for r in range(ROUNDS):
             last = r == ROUNDS - 1

@@ -28,14 +28,14 @@ K_PASS = 4 * P
 PASSES = HID // K_PASS
 PASS_WORDS = K_PASS // 2
 HALF = HEADS * ROT
+MINUS_SIN, COS, SIN = 0, 1, 2
 PLAIN, ROTATED = 0, 1
 ROUND = 2
 ROUNDS = TILES // ROUND
 PSUM_BANKS = 8
 STORE_HALVES = [slice(0, HEADS // 2), slice(HEADS // 2, HEADS)]
 EARLY_TILES = 4
-WARM_FIRST, WARM_BETWEEN = 4, 1
-AHEAD = 2
+WARM_FIRST, WARM_BETWEEN = 3, 2
 BASE_PAIRS = 8
 ROUND_MAGIC = 12582912.0
 
@@ -58,16 +58,17 @@ def tile_deepseekv4attention_pb_kernel(tc, hidden, wq_words, wq_scales, out):
         w_raw = keep.tile([P, PASSES * 2 * HID], U8, name="w_raw")
         s_raw = keep.tile([P, PASSES * HID], U8, name="s_raw")
 
-        nc.vector.memset(s_raw[:].bitcast(I32), 0)
-        for j in range(ROUND):
-            nc.sync.dma_start(out=x_sb[0][:, j, :], in_=x_rows[:, j, :])
-        nc.sync.dma_start(out=x_sb[1][:], in_=x_rows[:, ROUND : 2 * ROUND, :])
+        nc.vector.memset(s_raw[:, 0:HID].bitcast(I32), 0)
+        nc.gpsimd.memset(s_raw[:, HID : 2 * HID].bitcast(I32), 0)
+        nc.sync.dma_start(out=x_sb[0][:, 0, :], in_=x_rows[:, 0, :])
         scale_rows = wq_scales.bitcast(I32).rearrange("g q n -> q g n")
         for quad in range(4):
             nc.sync.dma_start(
                 out=s_raw[32 * quad : 32 * quad + 4, :].bitcast(I32).rearrange("q (g n) -> q g n", g=PASSES),
                 in_=scale_rows[4 * quad : 4 * quad + 4],
             )
+        nc.sync.dma_start(out=x_sb[0][:, 1, :], in_=x_rows[:, 1, :])
+        nc.sync.dma_start(out=x_sb[1][:], in_=x_rows[:, ROUND : 2 * ROUND, :])
         nc.sync.dma_start(
             out=w_raw[:].bitcast(I32).rearrange("p (g n) -> p g n", g=PASSES),
             in_=wq_words.bitcast(I32).rearrange("g p n -> p g n"),
@@ -77,15 +78,14 @@ def tile_deepseekv4attention_pb_kernel(tc, hidden, wq_words, wq_scales, out):
 
         token = keep.tile([P, TILES], I32, name="token")
         nc.gpsimd.iota(token[:], pattern=[[1, TILES]], base=0, channel_multiplier=TILES)
+        zeros = keep.tile([P, HALF], BF16, name="zeros")
+        nc.gpsimd.memset(zeros[:].bitcast(I32), 0)
         ident = keep.tile([P, P], F32, name="ident")
         make_identity(nc, ident[:])
 
         first_sin = keep.tile([P, 1], F32, name="first_sin")
         nc.gpsimd.memset(first_sin[:], 0.0)
         nc.scalar.activation(out=first_sin[:], in_=first_sin[:], func=ACT.Sin)
-
-        zeros = keep.tile([P, HALF], BF16, name="zeros")
-        nc.gpsimd.memset(zeros[:].bitcast(I32), 0)
 
         turns = keep.tile([P, TILES, PAIRS], F32, name="turns")
         for i in range(BASE_PAIRS):
@@ -106,27 +106,24 @@ def tile_deepseekv4attention_pb_kernel(tc, hidden, wq_words, wq_scales, out):
         nc.vector.tensor_scalar(
             out=whole[:], in0=turns[:], scalar1=ROUND_MAGIC, scalar2=ROUND_MAGIC, op0=ALU.add, op1=ALU.subtract
         )
-        sin_turn = keep.tile([P, TILES, PAIRS], F32, name="sin_turn")
-        nc.vector.tensor_tensor(out=sin_turn[:], in0=turns[:], in1=whole[:], op=ALU.subtract)
+        planes = keep.tile([P, 3, TILES, PAIRS], F32, name="planes")
+        nc.vector.tensor_tensor(out=planes[:, SIN], in0=turns[:], in1=whole[:], op=ALU.subtract)
         wraps = keep.tile([P, TILES, PAIRS], F32, name="wraps")
-        nc.vector.tensor_scalar(out=wraps[:], in0=sin_turn[:], scalar1=0.25, scalar2=None, op0=ALU.is_gt)
-        cos_turn = keep.tile([P, TILES, PAIRS], F32, name="cos_turn")
+        nc.vector.tensor_scalar(out=wraps[:], in0=planes[:, SIN], scalar1=0.25, scalar2=None, op0=ALU.is_gt)
+        nc.vector.tensor_scalar(out=planes[:, MINUS_SIN], in0=planes[:, SIN], scalar1=-1.0, scalar2=None, op0=ALU.mult)
         nc.vector.scalar_tensor_tensor(
-            out=cos_turn[:], in0=sin_turn[:], scalar=0.25, in1=wraps[:], op0=ALU.add, op1=ALU.subtract
+            out=planes[:, COS], in0=planes[:, SIN], scalar=0.25, in1=wraps[:], op0=ALU.add, op1=ALU.subtract
         )
-        table = keep.tile([P, TILES, 4, PAIRS], F32, name="table")
+        table = keep.tile([P, TILES, 2, PAIRS, 2], F32, name="table")
 
-        def sin_planes(tiles):
-            nc.scalar.activation(out=table[:, tiles, 1, :], in_=sin_turn[:, tiles, :], func=ACT.Sin, scale=-TWO_PI)
-            nc.scalar.activation(out=table[:, tiles, 2, :], in_=sin_turn[:, tiles, :], func=ACT.Sin, scale=TWO_PI)
-
-        def cos_planes(tiles):
-            nc.scalar.activation(
-                out=table[:, tiles, 0:4:3, :],
-                in_=cos_turn[:, tiles, :].unsqueeze(2).to_broadcast([P, tiles.stop - tiles.start, 2, PAIRS]),
-                func=ACT.Sin,
-                scale=TWO_PI,
-            )
+        def make_factors(tiles):
+            for e in range(2):
+                nc.scalar.activation(
+                    out=table[:, tiles, e],
+                    in_=planes[:, 1 - e : 3 - e, tiles, :].rearrange("p o j i -> p j i o"),
+                    func=ACT.Sin,
+                    scale=TWO_PI,
+                )
 
         early, late = slice(0, EARLY_TILES), slice(EARLY_TILES, TILES)
 
@@ -145,7 +142,7 @@ def tile_deepseekv4attention_pb_kernel(tc, hidden, wq_words, wq_scales, out):
                         .rearrange("p (h f c) -> p f h c", f=2, h=HEADS)[:, half],
                     )
 
-        xt_of, grouped_of, codes_of, planes_of, acc_of, res_of = {}, {}, {}, {}, {}, {}
+        xt_of, grouped_of, codes_of, scales_of, acc_of, res_of = {}, {}, {}, {}, {}, {}
 
         warm = acc_pool.tile([P, HALF], F32, name="acc")
 
@@ -153,19 +150,31 @@ def tile_deepseekv4attention_pb_kernel(tc, hidden, wq_words, wq_scales, out):
             for turn in range(count):
                 nc.tensor.matmul(warm[:], lhsT=zeros[:, 0:P], rhs=zeros[:], start=True, stop=True)
 
+        lined_up = {}
+
+        def line_up(r):
+            words = stage.tile([P, PASSES, 2, P], F32, name="words", bufs=2)
+            nc.scalar.copy(
+                out=words[:],
+                in_=x_sb[r][:, 1, :].bitcast(F32).rearrange("p (g w u) -> p g u w", g=PASSES, u=2),
+            )
+            lined_up[r] = words
+
         def transposes(r):
             for a in range(ROUND):
                 words = x_sb[r][:, a, :].bitcast(F32)
                 xt = xt_pool.tile([P, 2 * PASSES, P], F32, name="xt")
                 for g in range(PASSES):
                     for u in range(2):
-                        nc.tensor.transpose(
-                            xt[:, 2 * g + u, :], words[:, PASS_WORDS * g + u : PASS_WORDS * (g + 1) : 2], ident[:]
-                        )
+                        if a == 1 and r in lined_up:
+                            in_ = lined_up[r][:, g, u, :]
+                        else:
+                            in_ = words[:, PASS_WORDS * g + u : PASS_WORDS * (g + 1) : 2]
+                        nc.tensor.transpose(xt[:, 2 * g + u, :], in_, ident[:])
                 xt_of[r, a] = xt
 
         def regroup(r):
-            grouped = stage.tile([P, ROUND * HID], BF16, name="grouped", align_bytes=64, bufs=AHEAD + 1)
+            grouped = stage.tile([P, ROUND * HID], BF16, name="grouped", align_bytes=64, bufs=2)
             for a in range(ROUND):
                 nc.scalar.copy(
                     out=grouped[:, a * HID : (a + 1) * HID].bitcast(F32).rearrange("p (g t u) -> p g t u", g=PASSES, u=2),
@@ -175,9 +184,9 @@ def tile_deepseekv4attention_pb_kernel(tc, hidden, wq_words, wq_scales, out):
 
         def quantise(r):
             codes = stage.tile([P, ROUND * PASSES * P], U32, name="codes", align_bytes=64, bufs=4)
-            planes = stage.tile([P, ROUND * PASSES * P], U8, name="planes", align_bytes=64, bufs=4)
-            nc.vector.quantize_mx(out=codes[:].bitcast(FP8X4), scales=planes[:], in_=grouped_of[r][:])
-            codes_of[r], planes_of[r] = codes, planes
+            scales = stage.tile([P, ROUND * PASSES * P], U8, name="scales", align_bytes=64, bufs=4)
+            nc.vector.quantize_mx(out=codes[:].bitcast(FP8X4), scales=scales[:], in_=grouped_of[r][:])
+            codes_of[r], scales_of[r] = codes, scales
 
         def matmuls(r, half):
             for a in range(ROUND):
@@ -188,7 +197,7 @@ def tile_deepseekv4attention_pb_kernel(tc, hidden, wq_words, wq_scales, out):
                     nc.tensor.matmul_mx(
                         out=acc[:],
                         lhsT=codes_of[r][:, tok].bitcast(FP8X4),
-                        lhsT_scale=planes_of[r][:, tok],
+                        lhsT_scale=scales_of[r][:, tok],
                         rhs=w_words[:, col * 2 * HALF : (col + 1) * 2 * HALF].bitcast(FP4X4),
                         rhs_scale=w_scales[:, col * HALF : (col + 1) * HALF],
                         start=(g == 0),
@@ -204,7 +213,7 @@ def tile_deepseekv4attention_pb_kernel(tc, hidden, wq_words, wq_scales, out):
                 products_of[r, a] = stage.tile([P, 2, HEADS, PAIRS, 2], F32, name="products", bufs=6)
             shape = [P, heads.stop - heads.start, PAIRS, 2]
             inputs = acc_of[r, a, ROTATED][:].rearrange("p (h i e) -> p e h i", h=HEADS, e=2)
-            factors = table[:, ROUND * r + a, :, :].rearrange("p (o e) i -> p e i o", e=2)
+            factors = table[:, ROUND * r + a]
             for e in range(2):
                 nc.vector.tensor_tensor(
                     out=products_of[r, a][:, e, heads],
@@ -224,17 +233,18 @@ def tile_deepseekv4attention_pb_kernel(tc, hidden, wq_words, wq_scales, out):
         def rotate(r):
             for a in range(ROUND):
                 multiply(r, a, all_heads)
-                if a == 0 and r + 1 < ROUNDS - 1:
+                if a == 0:
                     quantise(r + 1)
                 add_products(nc.gpsimd, r, a, all_heads)
-            if r == ROUNDS - 3:
-                quantise(ROUNDS - 1)
 
         def rotate_last(r):
             for half in STORE_HALVES:
                 for a in range(ROUND):
                     multiply(r, a, half)
-                    add_products(nc.gpsimd if half == STORE_HALVES[0] else nc.vector, r, a, half)
+            for half in STORE_HALVES:
+                for a in range(ROUND):
+                    first = half == STORE_HALVES[0] and a == 0
+                    add_products(nc.gpsimd if first else nc.vector, r, a, half)
 
         def copy_plain(r):
             for a in range(ROUND):
@@ -250,28 +260,23 @@ def tile_deepseekv4attention_pb_kernel(tc, hidden, wq_words, wq_scales, out):
         transposes(0)
         warm_up(WARM_BETWEEN)
         regroup(0)
-        sin_planes(early)
-        cos_planes(early)
+        make_factors(early)
         quantise(0)
         order_columns(ROTATED)
         order_columns(PLAIN)
-        for r in range(1, AHEAD):
-            transposes(r)
-            warm_up(WARM_BETWEEN)
-            regroup(r)
         for r in range(ROUNDS):
             last = r == ROUNDS - 1
-            if r == 1:
-                sin_planes(late)
-                cos_planes(late)
             res_of[r] = stage.tile([P, HEADS, ROUND, HEAD_DIM], F32, name="res", bufs=4)
             if not last:
-                matmuls(r, ROTATED)
-            if r == ROUNDS - 2:
-                matmuls(r + 1, ROTATED)
-            if r + AHEAD < ROUNDS:
-                transposes(r + AHEAD)
-                regroup(r + AHEAD)
+                transposes(r + 1)
+                if r == 0:
+                    warm_up(WARM_BETWEEN)
+                regroup(r + 1)
+            if r + 2 < ROUNDS:
+                line_up(r + 2)
+            if r == 0:
+                make_factors(late)
+            matmuls(r, ROTATED)
             matmuls(r, PLAIN)
             if last:
                 rotate_last(r)

@@ -60,14 +60,14 @@ def tile_deepseekv4attention_pb_kernel(tc, hidden, wq_words, wq_scales, out):
 
         nc.vector.memset(s_raw[:, 0:HID].bitcast(I32), 0)
         nc.gpsimd.memset(s_raw[:, HID : 2 * HID].bitcast(I32), 0)
-        nc.sync.dma_start(out=x_sb[0][:, 0, :], in_=x_rows[:, 0, :])
+        for j in range(ROUND):
+            nc.sync.dma_start(out=x_sb[0][:, j, :], in_=x_rows[:, j, :])
         scale_rows = wq_scales.bitcast(I32).rearrange("g q n -> q g n")
         for quad in range(4):
             nc.sync.dma_start(
                 out=s_raw[32 * quad : 32 * quad + 4, :].bitcast(I32).rearrange("q (g n) -> q g n", g=PASSES),
                 in_=scale_rows[4 * quad : 4 * quad + 4],
             )
-        nc.sync.dma_start(out=x_sb[0][:, 1, :], in_=x_rows[:, 1, :])
         nc.sync.dma_start(out=x_sb[1][:], in_=x_rows[:, ROUND : 2 * ROUND, :])
         nc.sync.dma_start(
             out=w_raw[:].bitcast(I32).rearrange("p (g n) -> p g n", g=PASSES),
@@ -211,16 +211,15 @@ def tile_deepseekv4attention_pb_kernel(tc, hidden, wq_words, wq_scales, out):
         def multiply(r, a, heads):
             if (r, a) not in products_of:
                 products_of[r, a] = stage.tile([P, 2, HEADS, PAIRS, 2], F32, name="products", bufs=6)
-            shape = [P, heads.stop - heads.start, PAIRS, 2]
+            shape = [P, 2, heads.stop - heads.start, PAIRS, 2]
             inputs = acc_of[r, a, ROTATED][:].rearrange("p (h i e) -> p e h i", h=HEADS, e=2)
             factors = table[:, ROUND * r + a]
-            for e in range(2):
-                nc.vector.tensor_tensor(
-                    out=products_of[r, a][:, e, heads],
-                    in0=inputs[:, e, heads].unsqueeze(3).to_broadcast(shape),
-                    in1=factors[:, e].unsqueeze(1).to_broadcast(shape),
-                    op=ALU.mult,
-                )
+            nc.vector.tensor_tensor(
+                out=products_of[r, a][:, :, heads],
+                in0=inputs[:, :, heads].unsqueeze(4).to_broadcast(shape),
+                in1=factors.unsqueeze(2).to_broadcast(shape),
+                op=ALU.mult,
+            )
 
         def add_products(engine, r, a, heads):
             engine.tensor_tensor(
@@ -235,7 +234,8 @@ def tile_deepseekv4attention_pb_kernel(tc, hidden, wq_words, wq_scales, out):
                 multiply(r, a, all_heads)
                 if a == 0:
                     quantise(r + 1)
-                add_products(nc.gpsimd, r, a, all_heads)
+                quick = r == ROUNDS - 2 and a == ROUND - 1
+                add_products(nc.vector if quick else nc.gpsimd, r, a, all_heads)
 
         def rotate_last(r):
             for half in STORE_HALVES:
@@ -243,8 +243,7 @@ def tile_deepseekv4attention_pb_kernel(tc, hidden, wq_words, wq_scales, out):
                     multiply(r, a, half)
             for half in STORE_HALVES:
                 for a in range(ROUND):
-                    first = half == STORE_HALVES[0] and a == 0
-                    add_products(nc.gpsimd if first else nc.vector, r, a, half)
+                    add_products(nc.gpsimd if half == STORE_HALVES[0] else nc.vector, r, a, half)
 
         def copy_plain(r):
             for a in range(ROUND):

@@ -35,7 +35,7 @@ ROUNDS = TILES // ROUND
 PSUM_BANKS = 8
 STORE_HALVES = [slice(0, HEADS // 2), slice(HEADS // 2, HEADS)]
 EARLY_TILES = 4
-WARM_FIRST, WARM_BETWEEN = 3, 2
+WARM_FIRST, WARM_BETWEEN = 4, 2
 BASE_PAIRS = 8
 ROUND_MAGIC = 12582912.0
 
@@ -152,13 +152,13 @@ def tile_deepseekv4attention_pb_kernel(tc, hidden, wq_words, wq_scales, out):
 
         lined_up = {}
 
-        def line_up(r):
-            words = stage.tile([P, PASSES, 2, P], F32, name="words", bufs=2)
+        def line_up(r, a):
+            words = stage.tile([P, PASSES, 2, P], F32, name="words", bufs=4)
             nc.scalar.copy(
                 out=words[:],
-                in_=x_sb[r][:, 1, :].bitcast(F32).rearrange("p (g w u) -> p g u w", g=PASSES, u=2),
+                in_=x_sb[r][:, a, :].bitcast(F32).rearrange("p (g w u) -> p g u w", g=PASSES, u=2),
             )
-            lined_up[r] = words
+            lined_up[r, a] = words
 
         def transposes(r):
             for a in range(ROUND):
@@ -166,8 +166,8 @@ def tile_deepseekv4attention_pb_kernel(tc, hidden, wq_words, wq_scales, out):
                 xt = xt_pool.tile([P, 2 * PASSES, P], F32, name="xt")
                 for g in range(PASSES):
                     for u in range(2):
-                        if a == 1 and r in lined_up:
-                            in_ = lined_up[r][:, g, u, :]
+                        if (r, a) in lined_up:
+                            in_ = lined_up[r, a][:, g, u, :]
                         else:
                             in_ = words[:, PASS_WORDS * g + u : PASS_WORDS * (g + 1) : 2]
                         nc.tensor.transpose(xt[:, 2 * g + u, :], in_, ident[:])
@@ -238,12 +238,15 @@ def tile_deepseekv4attention_pb_kernel(tc, hidden, wq_words, wq_scales, out):
                 add_products(nc.vector if quick else nc.gpsimd, r, a, all_heads)
 
         def rotate_last(r):
-            for half in STORE_HALVES:
-                for a in range(ROUND):
-                    multiply(r, a, half)
-            for half in STORE_HALVES:
-                for a in range(ROUND):
-                    add_products(nc.gpsimd if half == STORE_HALVES[0] else nc.vector, r, a, half)
+            first, second = STORE_HALVES
+            multiply(r, 0, first)
+            multiply(r, 1, first)
+            multiply(r, 0, second)
+            add_products(nc.gpsimd, r, 0, first)
+            add_products(nc.vector, r, 1, first)
+            multiply(r, 1, second)
+            add_products(nc.gpsimd, r, 0, second)
+            add_products(nc.vector, r, 1, second)
 
         def copy_plain(r):
             for a in range(ROUND):
@@ -272,7 +275,9 @@ def tile_deepseekv4attention_pb_kernel(tc, hidden, wq_words, wq_scales, out):
                     warm_up(WARM_BETWEEN)
                 regroup(r + 1)
             if r + 2 < ROUNDS:
-                line_up(r + 2)
+                if r in (3, 5):
+                    line_up(r + 2, 0)
+                line_up(r + 2, 1)
             if r == 0:
                 make_factors(late)
             matmuls(r, ROTATED)

@@ -27,13 +27,14 @@ TILES = TOKENS // P
 K_PASS = 4 * P
 PASSES = HID // K_PASS
 PASS_WORDS = K_PASS // 2
-HALF = HEADS * ROT
+HALF_HEADS = HEADS // 2
+HALF = HALF_HEADS * HEAD_DIM
 MINUS_SIN, COS, SIN = 0, 1, 2
-PLAIN, ROTATED = 0, 1
 ROUND = 2
 ROUNDS = TILES // ROUND
+GROUP = 4
+GROUPS = TILES // GROUP
 PSUM_BANKS = 8
-STORE_HALVES = [slice(0, HEADS // 2), slice(HEADS // 2, HEADS)]
 EARLY_TILES = 4
 WARM_FIRST, WARM_BETWEEN = 4, 2
 BASE_PAIRS = 8
@@ -55,22 +56,22 @@ def tile_deepseekv4attention_pb_kernel(tc, hidden, wq_words, wq_scales, out):
         stack.enter_context(tc.manual_schedule())
 
         x_sb = [keep.tile([P, ROUND, HID], BF16, name="x%d" % r) for r in range(ROUNDS)]
-        w_raw = keep.tile([P, PASSES * 2 * HID], U8, name="w_raw")
-        s_raw = keep.tile([P, PASSES * HID], U8, name="s_raw")
+        w_words = keep.tile([P, PASSES * 2 * HID], U8, name="w_words", align_bytes=64)
+        w_scales = keep.tile([P, PASSES * HID], U8, name="w_scales", align_bytes=64)
 
-        nc.vector.memset(s_raw[:, 0:HID].bitcast(I32), 0)
-        nc.gpsimd.memset(s_raw[:, HID : 2 * HID].bitcast(I32), 0)
+        nc.vector.memset(w_scales[:, 0:HID].bitcast(I32), 0)
+        nc.gpsimd.memset(w_scales[:, HID : 2 * HID].bitcast(I32), 0)
         for j in range(ROUND):
             nc.sync.dma_start(out=x_sb[0][:, j, :], in_=x_rows[:, j, :])
         scale_rows = wq_scales.bitcast(I32).rearrange("g q n -> q g n")
         for quad in range(4):
             nc.sync.dma_start(
-                out=s_raw[32 * quad : 32 * quad + 4, :].bitcast(I32).rearrange("q (g n) -> q g n", g=PASSES),
+                out=w_scales[32 * quad : 32 * quad + 4, :].bitcast(I32).rearrange("q (g n) -> q g n", g=PASSES),
                 in_=scale_rows[4 * quad : 4 * quad + 4],
             )
         nc.sync.dma_start(out=x_sb[1][:], in_=x_rows[:, ROUND : 2 * ROUND, :])
         nc.sync.dma_start(
-            out=w_raw[:].bitcast(I32).rearrange("p (g n) -> p g n", g=PASSES),
+            out=w_words[:].bitcast(I32).rearrange("p (g n) -> p g n", g=PASSES),
             in_=wq_words.bitcast(I32).rearrange("g p n -> p g n"),
         )
         for r in range(2, ROUNDS):
@@ -116,7 +117,8 @@ def tile_deepseekv4attention_pb_kernel(tc, hidden, wq_words, wq_scales, out):
         )
         table = keep.tile([P, TILES, 2, PAIRS, 2], F32, name="table")
 
-        def make_factors(tiles):
+        def make_factors(q):
+            tiles = slice(GROUP * q, GROUP * (q + 1))
             for e in range(2):
                 nc.scalar.activation(
                     out=table[:, tiles, e],
@@ -124,23 +126,6 @@ def tile_deepseekv4attention_pb_kernel(tc, hidden, wq_words, wq_scales, out):
                     func=ACT.Sin,
                     scale=TWO_PI,
                 )
-
-        early, late = slice(0, EARLY_TILES), slice(EARLY_TILES, TILES)
-
-        w_words = keep.tile([P, PASSES * 2 * HID], U8, name="w_words", align_bytes=64)
-        w_scales = keep.tile([P, PASSES * HID], U8, name="w_scales", align_bytes=64)
-
-        def order_columns(half):
-            for g in range(PASSES):
-                for raw, ordered in ((w_raw, w_words), (s_raw, w_scales)):
-                    width = raw.shape[1] // (2 * PASSES)
-                    col = g * 2 + half
-                    nc.vector.tensor_copy(
-                        out=ordered[:, col * width : (col + 1) * width].bitcast(I32).rearrange("p (h c) -> p h c", h=HEADS),
-                        in_=raw[:, g * 2 * width : (g + 1) * 2 * width]
-                        .bitcast(I32)
-                        .rearrange("p (h f c) -> p f h c", f=2, h=HEADS)[:, half],
-                    )
 
         xt_of, grouped_of, codes_of, scales_of, acc_of, res_of = {}, {}, {}, {}, {}, {}
 
@@ -152,9 +137,9 @@ def tile_deepseekv4attention_pb_kernel(tc, hidden, wq_words, wq_scales, out):
 
         lined_up = {}
 
-        def line_up(r, a):
-            words = stage.tile([P, PASSES, 2, P], F32, name="words", bufs=4)
-            nc.scalar.copy(
+        def line_up(r, a, copy=nc.scalar.copy):
+            words = stage.tile([P, PASSES, 2, P], F32, name="words", bufs=6)
+            copy(
                 out=words[:],
                 in_=x_sb[r][:, a, :].bitcast(F32).rearrange("p (g w u) -> p g u w", g=PASSES, u=2),
             )
@@ -183,12 +168,12 @@ def tile_deepseekv4attention_pb_kernel(tc, hidden, wq_words, wq_scales, out):
             grouped_of[r] = grouped
 
         def quantise(r):
-            codes = stage.tile([P, ROUND * PASSES * P], U32, name="codes", align_bytes=64, bufs=4)
-            scales = stage.tile([P, ROUND * PASSES * P], U8, name="scales", align_bytes=64, bufs=4)
+            codes = stage.tile([P, ROUND * PASSES * P], U32, name="codes", align_bytes=64, bufs=5)
+            scales = stage.tile([P, ROUND * PASSES * P], U8, name="scales", align_bytes=64, bufs=5)
             nc.vector.quantize_mx(out=codes[:].bitcast(FP8X4), scales=scales[:], in_=grouped_of[r][:])
             codes_of[r], scales_of[r] = codes, scales
 
-        def matmuls(r, half):
+        def matmuls(pair, half):
             for a in range(ROUND):
                 acc = acc_pool.tile([P, HALF], F32, name="acc")
                 for g in range(PASSES):
@@ -196,96 +181,126 @@ def tile_deepseekv4attention_pb_kernel(tc, hidden, wq_words, wq_scales, out):
                     col = g * 2 + half
                     nc.tensor.matmul_mx(
                         out=acc[:],
-                        lhsT=codes_of[r][:, tok].bitcast(FP8X4),
-                        lhsT_scale=scales_of[r][:, tok],
+                        lhsT=codes_of[pair][:, tok].bitcast(FP8X4),
+                        lhsT_scale=scales_of[pair][:, tok],
                         rhs=w_words[:, col * 2 * HALF : (col + 1) * 2 * HALF].bitcast(FP4X4),
                         rhs_scale=w_scales[:, col * HALF : (col + 1) * HALF],
                         start=(g == 0),
                         stop=(g == PASSES - 1),
                     )
-                acc_of[r, a, half] = acc
+                acc_of[pair, half, a] = acc
 
         products_of = {}
-        all_heads = slice(0, HEADS)
 
-        def multiply(r, a, heads):
-            if (r, a) not in products_of:
-                products_of[r, a] = stage.tile([P, 2, HEADS, PAIRS, 2], F32, name="products", bufs=6)
-            shape = [P, 2, heads.stop - heads.start, PAIRS, 2]
-            inputs = acc_of[r, a, ROTATED][:].rearrange("p (h i e) -> p e h i", h=HEADS, e=2)
-            factors = table[:, ROUND * r + a]
-            nc.vector.tensor_tensor(
-                out=products_of[r, a][:, :, heads],
-                in0=inputs[:, :, heads].unsqueeze(4).to_broadcast(shape),
-                in1=factors.unsqueeze(2).to_broadcast(shape),
-                op=ALU.mult,
-            )
+        all_heads = slice(0, HALF_HEADS)
 
-        def add_products(engine, r, a, heads):
+        def multiply(pair, half, a, heads=all_heads):
+            if (pair, half) not in products_of:
+                products_of[pair, half] = stage.tile([P, ROUND, 2, HALF_HEADS, PAIRS, 2], F32, name="products", bufs=4)
+            shape = [P, heads.stop - heads.start, PAIRS, 2]
+            inputs = acc_of[pair, half, a][:].rearrange("p (h f i e) -> p f e h i", h=HALF_HEADS, f=2, e=2)[:, 1, :, heads]
+            factors = table[:, ROUND * pair + a]
+            for e in range(2):
+                nc.vector.tensor_tensor(
+                    out=products_of[pair, half][:, a, e, heads],
+                    in0=inputs[:, e].unsqueeze(3).to_broadcast(shape),
+                    in1=factors[:, e].unsqueeze(1).to_broadcast(shape),
+                    op=ALU.mult,
+                )
+
+        def add_products(engine, pair, half, heads=all_heads):
+            products = products_of[pair, half]
             engine.tensor_tensor(
-                out=res_of[r][:, heads, a, HEAD_DIM - ROT : HEAD_DIM],
-                in0=products_of[r, a][:, 0, heads].rearrange("p h i o -> p h (i o)"),
-                in1=products_of[r, a][:, 1, heads].rearrange("p h i o -> p h (i o)"),
+                out=res_of[pair, half][:, heads, :, HEAD_DIM - ROT : HEAD_DIM].rearrange("p h a d -> p a h d"),
+                in0=products[:, :, 0, heads].rearrange("p a h i o -> p a h (i o)"),
+                in1=products[:, :, 1, heads].rearrange("p a h i o -> p a h (i o)"),
                 op=ALU.add,
             )
 
-        def rotate(r):
-            for a in range(ROUND):
-                multiply(r, a, all_heads)
-                if a == 0:
-                    quantise(r + 1)
-                quick = r == ROUNDS - 2 and a == ROUND - 1
-                add_products(nc.vector if quick else nc.gpsimd, r, a, all_heads)
+        def copy_plain(pair, half, a):
+            nc.scalar.copy(
+                out=res_of[pair, half][:, :, a, 0 : HEAD_DIM - ROT],
+                in_=acc_of[pair, half, a][:].rearrange("p (h f d) -> p f h d", h=HALF_HEADS, f=2)[:, 0],
+            )
 
-        def rotate_last(r):
-            first, second = STORE_HALVES
-            multiply(r, 0, first)
-            multiply(r, 1, first)
-            multiply(r, 0, second)
-            add_products(nc.gpsimd, r, 0, first)
-            add_products(nc.vector, r, 1, first)
-            multiply(r, 1, second)
-            add_products(nc.gpsimd, r, 0, second)
-            add_products(nc.vector, r, 1, second)
+        pieces = [(0, 0), (0, 1)] + [(r + b, half) for r in (1, 3, 5) for half in range(2) for b in range(2)] + [(7, 0), (7, 1)]
 
-        def copy_plain(r):
-            for a in range(ROUND):
-                nc.scalar.copy(
-                    out=res_of[r][:, :, a, 0 : HEAD_DIM - ROT],
-                    in_=acc_of[r, a, PLAIN][:].rearrange("p (h d) -> p h d", h=HEADS),
-                )
+        def open_unit(k):
+            unit = pieces[k : k + 2]
+            tiles = ROUND * len(set(pair for pair, half in unit))
+            res = stage.tile([P, 2 * ROUND * HALF_HEADS // tiles, tiles, HEAD_DIM], F32, name="res", bufs=4)
+            for n, (pair, half) in enumerate(unit):
+                if tiles == ROUND:
+                    res_of[pair, half] = res[:, HALF_HEADS * n : HALF_HEADS * (n + 1)]
+                else:
+                    res_of[pair, half] = res[:, :, ROUND * n : ROUND * (n + 1), :]
+            return res
 
-        def store(r, heads):
-            nc.sync.dma_start(out=out_rows[:, heads, ROUND * r : ROUND * (r + 1), :], in_=res_of[r][:, heads])
+        def store(res, first, last, heads=None):
+            (pair0, half0), (pair1, half1) = pieces[first], pieces[last]
+            cols = slice(HALF_HEADS * half0, HALF_HEADS * (half1 + 1))
+            if heads:
+                cols = slice(cols.start + heads.start, cols.start + heads.stop)
+                res = res[:, heads]
+            nc.sync.dma_start(out=out_rows[:, cols, ROUND * pair0 : ROUND * (pair1 + 1), :], in_=res)
 
         warm_up(WARM_FIRST)
         transposes(0)
         warm_up(WARM_BETWEEN)
         regroup(0)
-        make_factors(early)
+        make_factors(0)
         quantise(0)
-        order_columns(ROTATED)
-        order_columns(PLAIN)
-        for r in range(ROUNDS):
-            last = r == ROUNDS - 1
-            res_of[r] = stage.tile([P, HEADS, ROUND, HEAD_DIM], F32, name="res", bufs=4)
-            if not last:
-                transposes(r + 1)
-                if r == 0:
-                    warm_up(WARM_BETWEEN)
-                regroup(r + 1)
-            if r + 2 < ROUNDS:
-                if r in (3, 5):
-                    line_up(r + 2, 0)
-                line_up(r + 2, 1)
-            if r == 0:
-                make_factors(late)
-            matmuls(r, ROTATED)
-            matmuls(r, PLAIN)
+        transposes(1)
+        warm_up(1)
+        regroup(1)
+        quantise(1)
+        TR = {1: 2, 3: 3, 5: 4, 7: 5, 9: 6, 11: 7}
+        QU = {1: 2, 3: 3, 5: 4, 7: 5, 9: 6, 11: 7}
+        LU = {3: [(4, 1)], 5: [(5, 1)], 7: [(6, 1)], 9: [(7, 1)]}
+        FA = {0: 1, 4: 2, 7: 3}
+        VL = {}
+        VA = [13]
+        res_at = {}
+        PLAIN_FIRST = [14, 15]
+        def finish(k):
+            pair, half = pieces[k]
+            if k not in PLAIN_FIRST:
+                for a in range(ROUND):
+                    copy_plain(pair, half, a)
+            if k == len(pieces) - 2 or k == 13 and False:
+                store(res_of[pair, half], k, k)
+            elif k % 2 == 1 and k < len(pieces) - 1:
+                store(res_at[k - 1][:], k - 1, k)
+        for k, (pair, half) in enumerate(pieces):
+            last = k == len(pieces) - 1
+            if k % 2 == 0:
+                res_at[k] = open_unit(k)
+            if k in TR:
+                transposes(TR[k])
+                regroup(TR[k])
+            for r, a in LU.get(k, []):
+                line_up(r, a)
+            if k in FA:
+                make_factors(FA[k])
+            matmuls(pair, half)
+            if k > 0:
+                finish(k - 1)
+            if k in PLAIN_FIRST:
+                for a in range(ROUND):
+                    copy_plain(pair, half, a)
             if last:
-                rotate_last(r)
+                first, second = slice(0, 2), slice(2, 4)
+                for heads in (first, second):
+                    for a in range(ROUND):
+                        multiply(pair, half, a, heads)
+                    add_products(nc.gpsimd if heads == first else nc.vector, pair, half, heads)
+                    store(res_of[pair, half], k, k, heads)
             else:
-                rotate(r)
-            copy_plain(r)
-            for heads in STORE_HALVES if last else [all_heads]:
-                store(r, heads)
+                for a in range(ROUND):
+                    multiply(pair, half, a)
+                    if a == 1 and k in QU:
+                        quantise(QU[k])
+                    if a == 1:
+                        for r, b in VL.get(k, []):
+                            line_up(r, b, nc.vector.tensor_copy)
+                add_products(nc.vector if k in VA else nc.gpsimd, pair, half)

@@ -256,7 +256,7 @@ def tile_deepseekv4attention_pb_kernel(tc, hidden, wq_words, wq_scales, out):
         quantise(1)
         TR = {1: 2, 3: 3, 5: 4, 7: 5, 9: 6, 11: 7}
         QU = {1: 2, 3: 3, 5: 4, 7: 5, 9: 6, 11: 7}
-        LU = {3: [(4, 1)], 5: [(5, 1)], 7: [(6, 1)], 9: [(7, 1)]}
+        LU = {}
         FA = {0: 1, 4: 2, 7: 3}
         VL = {}
         VA = [13]

@@ -59,8 +59,7 @@ def tile_deepseekv4attention_pb_kernel(tc, hidden, wq_words, wq_scales, out):
         w_words = keep.tile([P, PASSES * 2 * HID], U8, name="w_words", align_bytes=64)
         w_scales = keep.tile([P, PASSES * HID], U8, name="w_scales", align_bytes=64)
 
-        nc.vector.memset(w_scales[:, 0:HID].bitcast(I32), 0)
-        nc.gpsimd.memset(w_scales[:, HID : 2 * HID].bitcast(I32), 0)
+        nc.vector.memset(w_scales[:].bitcast(I32), 0)
         for j in range(ROUND):
             nc.sync.dma_start(out=x_sb[0][:, j, :], in_=x_rows[:, j, :])
         scale_rows = wq_scales.bitcast(I32).rearrange("g q n -> q g n")
@@ -69,23 +68,22 @@ def tile_deepseekv4attention_pb_kernel(tc, hidden, wq_words, wq_scales, out):
                 out=w_scales[32 * quad : 32 * quad + 4, :].bitcast(I32).rearrange("q (g n) -> q g n", g=PASSES),
                 in_=scale_rows[4 * quad : 4 * quad + 4],
             )
-        nc.sync.dma_start(out=x_sb[1][:], in_=x_rows[:, ROUND : 2 * ROUND, :])
         nc.sync.dma_start(
             out=w_words[:].bitcast(I32).rearrange("p (g n) -> p g n", g=PASSES),
             in_=wq_words.bitcast(I32).rearrange("g p n -> p g n"),
         )
-        for r in range(2, ROUNDS):
+        for r in range(1, ROUNDS):
             nc.sync.dma_start(out=x_sb[r][:], in_=x_rows[:, ROUND * r : ROUND * (r + 1), :])
 
         token = keep.tile([P, TILES], I32, name="token")
         nc.gpsimd.iota(token[:], pattern=[[1, TILES]], base=0, channel_multiplier=TILES)
         zeros = keep.tile([P, HALF], BF16, name="zeros")
-        nc.gpsimd.memset(zeros[:].bitcast(I32), 0)
+        nc.vector.memset(zeros[:].bitcast(I32), 0)
         ident = keep.tile([P, P], F32, name="ident")
         make_identity(nc, ident[:])
 
         first_sin = keep.tile([P, 1], F32, name="first_sin")
-        nc.gpsimd.memset(first_sin[:], 0.0)
+        nc.vector.memset(first_sin[:], 0.0)
         nc.scalar.activation(out=first_sin[:], in_=first_sin[:], func=ACT.Sin)
 
         turns = keep.tile([P, TILES, PAIRS], F32, name="turns")
@@ -112,9 +110,12 @@ def tile_deepseekv4attention_pb_kernel(tc, hidden, wq_words, wq_scales, out):
         wraps = keep.tile([P, TILES, PAIRS], F32, name="wraps")
         nc.vector.tensor_scalar(out=wraps[:], in0=planes[:, SIN], scalar1=0.25, scalar2=None, op0=ALU.is_gt)
         nc.vector.tensor_scalar(out=planes[:, MINUS_SIN], in0=planes[:, SIN], scalar1=-1.0, scalar2=None, op0=ALU.mult)
-        nc.vector.scalar_tensor_tensor(
-            out=planes[:, COS], in0=planes[:, SIN], scalar=0.25, in1=wraps[:], op0=ALU.add, op1=ALU.subtract
-        )
+
+        def make_cosines():
+            nc.vector.scalar_tensor_tensor(
+                out=planes[:, COS], in0=planes[:, SIN], scalar=0.25, in1=wraps[:], op0=ALU.add, op1=ALU.subtract
+            )
+
         table = keep.tile([P, TILES, 2, PAIRS, 2], F32, name="table")
 
         def make_factors(q):
@@ -167,11 +168,16 @@ def tile_deepseekv4attention_pb_kernel(tc, hidden, wq_words, wq_scales, out):
                 )
             grouped_of[r] = grouped
 
-        def quantise(r):
-            codes = stage.tile([P, ROUND * PASSES * P], U32, name="codes", align_bytes=64, bufs=5)
-            scales = stage.tile([P, ROUND * PASSES * P], U8, name="scales", align_bytes=64, bufs=5)
-            nc.vector.quantize_mx(out=codes[:].bitcast(FP8X4), scales=scales[:], in_=grouped_of[r][:])
-            codes_of[r], scales_of[r] = codes, scales
+        def quantise(r, first=0, last=ROUND):
+            if first == 0:
+                codes_of[r] = stage.tile([P, ROUND * PASSES * P], U32, name="codes", align_bytes=64, bufs=5)
+                scales_of[r] = stage.tile([P, ROUND * PASSES * P], U8, name="scales", align_bytes=64, bufs=5)
+            words = slice(first * PASSES * P, last * PASSES * P)
+            nc.vector.quantize_mx(
+                out=codes_of[r][:, words].bitcast(FP8X4),
+                scales=scales_of[r][:, words],
+                in_=grouped_of[r][:, first * HID : last * HID],
+            )
 
         def matmuls(pair, half):
             for a in range(ROUND):
@@ -223,7 +229,7 @@ def tile_deepseekv4attention_pb_kernel(tc, hidden, wq_words, wq_scales, out):
                 in_=acc_of[pair, half, a][:].rearrange("p (h f d) -> p f h d", h=HALF_HEADS, f=2)[:, 0],
             )
 
-        pieces = [(0, 0), (0, 1)] + [(r + b, half) for r in (1, 3, 5) for half in range(2) for b in range(2)] + [(7, 0), (7, 1)]
+        pieces = [(r, half) for r in range(6) for half in range(2)] + [(6, 0), (7, 0), (6, 1), (7, 1)]
 
         def open_unit(k):
             unit = pieces[k : k + 2]
@@ -244,22 +250,23 @@ def tile_deepseekv4attention_pb_kernel(tc, hidden, wq_words, wq_scales, out):
                 res = res[:, heads]
             nc.sync.dma_start(out=out_rows[:, cols, ROUND * pair0 : ROUND * (pair1 + 1), :], in_=res)
 
-        warm_up(WARM_FIRST)
+        warm_up(3)
         transposes(0)
-        warm_up(WARM_BETWEEN)
+        warm_up(2)
         regroup(0)
+        quantise(0, 0, 1)
+        make_cosines()
+        quantise(0, 1, 2)
         make_factors(0)
-        quantise(0)
-        transposes(1)
-        warm_up(1)
-        regroup(1)
-        quantise(1)
-        TR = {1: 2, 3: 3, 5: 4, 7: 5, 9: 6, 11: 7}
-        QU = {1: 2, 3: 3, 5: 4, 7: 5, 9: 6, 11: 7}
+        TR = {1: 1, 2: 2, 4: 3, 6: 4, 8: 5, 10: 6, 11: 7}
+        QU = {1: 1, 2: 2, 4: 3, 6: 4, 8: 5, 10: 6, 11: 7}
         LU = {}
-        FA = {0: 1, 4: 2, 7: 3}
+        FA = {2: 1, 6: 2, 10: 3}
         VL = {}
-        VA = [13]
+        QA = {1: 0}
+        SPLIT = []
+        SINGLE = [10, 11]
+        VA = [0, 13]
         res_at = {}
         PLAIN_FIRST = [14, 15]
         def finish(k):
@@ -267,7 +274,9 @@ def tile_deepseekv4attention_pb_kernel(tc, hidden, wq_words, wq_scales, out):
             if k not in PLAIN_FIRST:
                 for a in range(ROUND):
                     copy_plain(pair, half, a)
-            if k == len(pieces) - 2 or k == 13 and False:
+            if k == len(pieces) - 2:
+                pass
+            elif k in SINGLE:
                 store(res_of[pair, half], k, k)
             elif k % 2 == 1 and k < len(pieces) - 1:
                 store(res_at[k - 1][:], k - 1, k)
@@ -293,14 +302,21 @@ def tile_deepseekv4attention_pb_kernel(tc, hidden, wq_words, wq_scales, out):
                 for heads in (first, second):
                     for a in range(ROUND):
                         multiply(pair, half, a, heads)
-                    add_products(nc.gpsimd if heads == first else nc.vector, pair, half, heads)
-                    store(res_of[pair, half], k, k, heads)
+                    add_products(nc.vector, *pieces[k - 1], heads)
+                    add_products(nc.vector, pair, half, heads)
+                    store(res_at[k - 1], k - 1, k, heads)
             else:
                 for a in range(ROUND):
                     multiply(pair, half, a)
-                    if a == 1 and k in QU:
+                    if a == QA.get(k, 1) and k in QU:
                         quantise(QU[k])
                     if a == 1:
                         for r, b in VL.get(k, []):
                             line_up(r, b, nc.vector.tensor_copy)
-                add_products(nc.vector if k in VA else nc.gpsimd, pair, half)
+                if k == len(pieces) - 2:
+                    pass
+                elif k in SPLIT:
+                    add_products(nc.vector, pair, half, slice(0, 1))
+                    add_products(nc.gpsimd, pair, half, slice(1, HALF_HEADS))
+                else:
+                    add_products(nc.vector if k in VA else nc.gpsimd, pair, half)

from contextlib import ExitStack

import concourse.mybir as mybir
from concourse.masks import make_identity

F32 = mybir.dt.float32
BF16 = mybir.dt.bfloat16
I32 = mybir.dt.int32
U32 = mybir.dt.uint32
U8 = mybir.dt.uint8
FP8X4 = mybir.dt.float8_e4m3fn_x4
FP4X4 = mybir.dt.float4_e2m1fn_x4
ALU = mybir.AluOpType
ACT = mybir.ActivationFunctionType

P = 128
TOKENS = 2048
HID = 1024
HEADS = 8
HEAD_DIM = 128
ROT = 64
PAIRS = ROT // 2
THETA = 10000.0
TWO_PI = 6.283185307179586

TILES = TOKENS // P
K_PASS = 4 * P
PASSES = HID // K_PASS
PASS_WORDS = K_PASS // 2
HALF_HEADS = HEADS // 2
HALF = HALF_HEADS * HEAD_DIM
MINUS_SIN, COS, SIN = 0, 1, 2
ROUND = 2
ROUNDS = TILES // ROUND
GROUP = 4
GROUPS = TILES // GROUP
PSUM_BANKS = 8
EARLY_TILES = 4
WARM_FIRST, WARM_BETWEEN = 4, 2
BASE_PAIRS = 8
ROUND_MAGIC = 12582912.0

FLOPS = 2 * TOKENS * HID * HEADS * HEAD_DIM


def tile_deepseekv4attention_pb_kernel(tc, hidden, wq_words, wq_scales, out):
    nc = tc.nc
    x_rows = hidden.flatten_outer_dims().rearrange("(p j) k -> p j k", j=TILES)
    out_rows = out.rearrange("b h t d -> (b h) t d").rearrange("h (p j) d -> p h j d", j=TILES)

    with ExitStack() as stack:
        keep = stack.enter_context(tc.tile_pool(name="keep", bufs=1))
        stage = stack.enter_context(tc.tile_pool(name="stage", bufs=3))
        xt_pool = stack.enter_context(tc.psum_pool(name="xt_pool", bufs=ROUND))
        acc_pool = stack.enter_context(tc.psum_pool(name="acc_pool", bufs=PSUM_BANKS - ROUND))
        stack.enter_context(tc.manual_schedule())

        x_sb = [keep.tile([P, ROUND, HID], BF16, name="x%d" % r) for r in range(ROUNDS)]
        w_words = keep.tile([P, PASSES * 2 * HID], U8, name="w_words", align_bytes=64)
        w_scales = keep.tile([P, PASSES * HID], U8, name="w_scales", align_bytes=64)

        nc.vector.memset(w_scales[:].bitcast(I32), 0)
        for j in range(ROUND):
            nc.sync.dma_start(out=x_sb[0][:, j, :], in_=x_rows[:, j, :])
        scale_rows = wq_scales.bitcast(I32).rearrange("g q n -> q g n")
        for quad in range(4):
            nc.sync.dma_start(
                out=w_scales[32 * quad : 32 * quad + 4, :].bitcast(I32).rearrange("q (g n) -> q g n", g=PASSES),
                in_=scale_rows[4 * quad : 4 * quad + 4],
            )
        nc.sync.dma_start(
            out=w_words[:].bitcast(I32).rearrange("p (g n) -> p g n", g=PASSES),
            in_=wq_words.bitcast(I32).rearrange("g p n -> p g n"),
        )
        for r in range(1, ROUNDS):
            nc.sync.dma_start(out=x_sb[r][:], in_=x_rows[:, ROUND * r : ROUND * (r + 1), :])

        token = keep.tile([P, TILES], I32, name="token")
        nc.gpsimd.iota(token[:], pattern=[[1, TILES]], base=0, channel_multiplier=TILES)
        zeros = keep.tile([P, HALF], BF16, name="zeros")
        nc.vector.memset(zeros[:].bitcast(I32), 0)
        ident = keep.tile([P, P], F32, name="ident")
        make_identity(nc, ident[:])

        first_sin = keep.tile([P, 1], F32, name="first_sin")
        nc.vector.memset(first_sin[:], 0.0)
        nc.scalar.activation(out=first_sin[:], in_=first_sin[:], func=ACT.Sin)

        turns = keep.tile([P, TILES, PAIRS], F32, name="turns")
        for i in range(BASE_PAIRS):
            nc.vector.tensor_scalar(
                out=turns[:, :, i], in0=token[:], scalar1=THETA ** (-i / PAIRS) / TWO_PI, scalar2=None, op0=ALU.mult
            )
        done = BASE_PAIRS
        while done < PAIRS:
            nc.vector.tensor_scalar(
                out=turns[:, :, done : 2 * done],
                in0=turns[:, :, 0:done],
                scalar1=THETA ** (-done / PAIRS),
                scalar2=None,
                op0=ALU.mult,
            )
            done *= 2
        whole = keep.tile([P, TILES, PAIRS], F32, name="whole")
        nc.vector.tensor_scalar(
            out=whole[:], in0=turns[:], scalar1=ROUND_MAGIC, scalar2=ROUND_MAGIC, op0=ALU.add, op1=ALU.subtract
        )
        planes = keep.tile([P, 3, TILES, PAIRS], F32, name="planes")
        nc.vector.tensor_tensor(out=planes[:, SIN], in0=turns[:], in1=whole[:], op=ALU.subtract)
        wraps = keep.tile([P, TILES, PAIRS], F32, name="wraps")
        nc.vector.tensor_scalar(out=wraps[:], in0=planes[:, SIN], scalar1=0.25, scalar2=None, op0=ALU.is_gt)
        nc.vector.tensor_scalar(out=planes[:, MINUS_SIN], in0=planes[:, SIN], scalar1=-1.0, scalar2=None, op0=ALU.mult)

        def make_cosines():
            nc.vector.scalar_tensor_tensor(
                out=planes[:, COS], in0=planes[:, SIN], scalar=0.25, in1=wraps[:], op0=ALU.add, op1=ALU.subtract
            )

        table = keep.tile([P, TILES, 2, PAIRS, 2], F32, name="table")

        def make_factors(q):
            tiles = slice(GROUP * q, GROUP * (q + 1))
            for e in range(2):
                nc.scalar.activation(
                    out=table[:, tiles, e],
                    in_=planes[:, 1 - e : 3 - e, tiles, :].rearrange("p o j i -> p j i o"),
                    func=ACT.Sin,
                    scale=TWO_PI,
                )

        xt_of, grouped_of, codes_of, scales_of, acc_of, res_of = {}, {}, {}, {}, {}, {}

        warm = acc_pool.tile([P, HALF], F32, name="acc")

        def warm_up(count):
            for turn in range(count):
                nc.tensor.matmul(warm[:], lhsT=zeros[:, 0:P], rhs=zeros[:], start=True, stop=True)

        lined_up = {}

        def line_up(r, a, copy=nc.scalar.copy):
            words = stage.tile([P, PASSES, 2, P], F32, name="words", bufs=6)
            copy(
                out=words[:],
                in_=x_sb[r][:, a, :].bitcast(F32).rearrange("p (g w u) -> p g u w", g=PASSES, u=2),
            )
            lined_up[r, a] = words

        def transposes(r):
            for a in range(ROUND):
                words = x_sb[r][:, a, :].bitcast(F32)
                xt = xt_pool.tile([P, 2 * PASSES, P], F32, name="xt")
                for g in range(PASSES):
                    for u in range(2):
                        if (r, a) in lined_up:
                            in_ = lined_up[r, a][:, g, u, :]
                        else:
                            in_ = words[:, PASS_WORDS * g + u : PASS_WORDS * (g + 1) : 2]
                        nc.tensor.transpose(xt[:, 2 * g + u, :], in_, ident[:])
                xt_of[r, a] = xt

        def regroup(r):
            grouped = stage.tile([P, ROUND * HID], BF16, name="grouped", align_bytes=64, bufs=2)
            for a in range(ROUND):
                nc.scalar.copy(
                    out=grouped[:, a * HID : (a + 1) * HID].bitcast(F32).rearrange("p (g t u) -> p g t u", g=PASSES, u=2),
                    in_=xt_of[r, a][:].rearrange("p (g u) t -> p g t u", u=2),
                )
            grouped_of[r] = grouped

        def quantise(r, first=0, last=ROUND):
            if first == 0:
                codes_of[r] = stage.tile([P, ROUND * PASSES * P], U32, name="codes", align_bytes=64, bufs=5)
                scales_of[r] = stage.tile([P, ROUND * PASSES * P], U8, name="scales", align_bytes=64, bufs=5)
            words = slice(first * PASSES * P, last * PASSES * P)
            nc.vector.quantize_mx(
                out=codes_of[r][:, words].bitcast(FP8X4),
                scales=scales_of[r][:, words],
                in_=grouped_of[r][:, first * HID : last * HID],
            )

        def matmuls(pair, half):
            for a in range(ROUND):
                acc = acc_pool.tile([P, HALF], F32, name="acc")
                for g in range(PASSES):
                    tok = slice((a * PASSES + g) * P, (a * PASSES + g + 1) * P)
                    col = g * 2 + half
                    nc.tensor.matmul_mx(
                        out=acc[:],
                        lhsT=codes_of[pair][:, tok].bitcast(FP8X4),
                        lhsT_scale=scales_of[pair][:, tok],
                        rhs=w_words[:, col * 2 * HALF : (col + 1) * 2 * HALF].bitcast(FP4X4),
                        rhs_scale=w_scales[:, col * HALF : (col + 1) * HALF],
                        start=(g == 0),
                        stop=(g == PASSES - 1),
                    )
                acc_of[pair, half, a] = acc

        products_of = {}

        all_heads = slice(0, HALF_HEADS)

        def multiply(pair, half, a, heads=all_heads):
            if (pair, half) not in products_of:
                products_of[pair, half] = stage.tile([P, ROUND, 2, HALF_HEADS, PAIRS, 2], F32, name="products", bufs=4)
            shape = [P, heads.stop - heads.start, PAIRS, 2]
            inputs = acc_of[pair, half, a][:].rearrange("p (h f i e) -> p f e h i", h=HALF_HEADS, f=2, e=2)[:, 1, :, heads]
            factors = table[:, ROUND * pair + a]
            for e in range(2):
                nc.vector.tensor_tensor(
                    out=products_of[pair, half][:, a, e, heads],
                    in0=inputs[:, e].unsqueeze(3).to_broadcast(shape),
                    in1=factors[:, e].unsqueeze(1).to_broadcast(shape),
                    op=ALU.mult,
                )

        def add_products(engine, pair, half, heads=all_heads):
            products = products_of[pair, half]
            engine.tensor_tensor(
                out=res_of[pair, half][:, heads, :, HEAD_DIM - ROT : HEAD_DIM].rearrange("p h a d -> p a h d"),
                in0=products[:, :, 0, heads].rearrange("p a h i o -> p a h (i o)"),
                in1=products[:, :, 1, heads].rearrange("p a h i o -> p a h (i o)"),
                op=ALU.add,
            )

        def copy_plain(pair, half, a):
            nc.scalar.copy(
                out=res_of[pair, half][:, :, a, 0 : HEAD_DIM - ROT],
                in_=acc_of[pair, half, a][:].rearrange("p (h f d) -> p f h d", h=HALF_HEADS, f=2)[:, 0],
            )

        pieces = [(r, half) for r in range(6) for half in range(2)] + [(6, 0), (7, 0), (6, 1), (7, 1)]

        def open_unit(k):
            unit = pieces[k : k + 2]
            tiles = ROUND * len(set(pair for pair, half in unit))
            res = stage.tile([P, 2 * ROUND * HALF_HEADS // tiles, tiles, HEAD_DIM], F32, name="res", bufs=4)
            for n, (pair, half) in enumerate(unit):
                if tiles == ROUND:
                    res_of[pair, half] = res[:, HALF_HEADS * n : HALF_HEADS * (n + 1)]
                else:
                    res_of[pair, half] = res[:, :, ROUND * n : ROUND * (n + 1), :]
            return res

        def store(res, first, last, heads=None):
            (pair0, half0), (pair1, half1) = pieces[first], pieces[last]
            cols = slice(HALF_HEADS * half0, HALF_HEADS * (half1 + 1))
            if heads:
                cols = slice(cols.start + heads.start, cols.start + heads.stop)
                res = res[:, heads]
            nc.sync.dma_start(out=out_rows[:, cols, ROUND * pair0 : ROUND * (pair1 + 1), :], in_=res)

        warm_up(3)
        transposes(0)
        warm_up(2)
        regroup(0)
        quantise(0, 0, 1)
        make_cosines()
        quantise(0, 1, 2)
        make_factors(0)
        TR = {1: 1, 2: 2, 4: 3, 6: 4, 8: 5, 10: 6, 11: 7}
        QU = {1: 1, 2: 2, 4: 3, 6: 4, 8: 5, 10: 6, 11: 7}
        LU = {}
        FA = {2: 1, 6: 2, 10: 3}
        VL = {}
        QA = {1: 0}
        SPLIT = []
        SINGLE = [10, 11]
        VA = [0, 13]
        res_at = {}
        PLAIN_FIRST = [14, 15]
        def finish(k):
            pair, half = pieces[k]
            if k not in PLAIN_FIRST:
                for a in range(ROUND):
                    copy_plain(pair, half, a)
            if k == len(pieces) - 2:
                pass
            elif k in SINGLE:
                store(res_of[pair, half], k, k)
            elif k % 2 == 1 and k < len(pieces) - 1:
                store(res_at[k - 1][:], k - 1, k)
        for k, (pair, half) in enumerate(pieces):
            last = k == len(pieces) - 1
            if k % 2 == 0:
                res_at[k] = open_unit(k)
            if k in TR:
                transposes(TR[k])
                regroup(TR[k])
            for r, a in LU.get(k, []):
                line_up(r, a)
            if k in FA:
                make_factors(FA[k])
            matmuls(pair, half)
            if k > 0:
                finish(k - 1)
            if k in PLAIN_FIRST:
                for a in range(ROUND):
                    copy_plain(pair, half, a)
            if last:
                first, second = slice(0, 2), slice(2, 4)
                for heads in (first, second):
                    for a in range(ROUND):
                        multiply(pair, half, a, heads)
                    add_products(nc.vector, *pieces[k - 1], heads)
                    add_products(nc.vector, pair, half, heads)
                    store(res_at[k - 1], k - 1, k, heads)
            else:
                for a in range(ROUND):
                    multiply(pair, half, a)
                    if a == QA.get(k, 1) and k in QU:
                        quantise(QU[k])
                    if a == 1:
                        for r, b in VL.get(k, []):
                            line_up(r, b, nc.vector.tensor_copy)
                if k == len(pieces) - 2:
                    pass
                elif k in SPLIT:
                    add_products(nc.vector, pair, half, slice(0, 1))
                    add_products(nc.gpsimd, pair, half, slice(1, HALF_HEADS))
                else:
                    add_products(nc.vector if k in VA else nc.gpsimd, pair, half)
